import numpy as np
import ml_dtypes


def mxq(x, axis, fmt="e4m3"):
    dtype, down = {"e4m3": (ml_dtypes.float8_e4m3fn, 7), "e5m2": (ml_dtypes.float8_e5m2, 14)}[fmt]
    v = np.moveaxis(np.asarray(x, np.float32).astype(ml_dtypes.bfloat16).astype(np.float64), axis, -1)
    blocks = v.reshape(v.shape[:-1] + (-1, 32))
    amax = np.abs(blocks).max(-1, keepdims=True)
    byte = np.maximum(np.where(amax > 0, np.frexp(amax)[1] - 1 + 127, 0) - down, 1)
    scale = np.exp2(byte - 127.0)
    codes = (blocks / scale).astype(np.float32).astype(dtype).astype(np.float64)
    return np.moveaxis((codes * scale).reshape(v.shape), -1, axis)


WIDE = False


def mx_kscale(k):
    if not WIDE:
        return np.ones(k)
    levels = np.array([10, -10, 5, -5, 0])
    a = np.random.permutation(np.resize(levels, k // 512 * 4)).reshape(k // 512, 4)
    idx = np.arange(k)
    return np.exp2(a[idx // 512, idx % 128 // 32])


BF16 = ml_dtypes.bfloat16


def bf(x):
    return np.asarray(x, np.float32).astype(BF16)


def f64(x):
    return np.asarray(x).astype(np.float64)


E2M1 = np.array([0.0, 0.5, 1.0, 1.5, 2.0, 3.0, 4.0, 6.0, -0.0, -0.5, -1.0, -1.5, -2.0, -3.0, -4.0, -6.0])


def pack_weight(w, fmt):
    k, n = w.shape
    w = f64(bf(w)).reshape(k // 32, 32, n)
    amax = np.abs(w).max(1)
    if fmt == "e4m3":
        byte = np.frexp(amax)[1] - 1 + 127 - 7
    else:
        mant, ex = np.frexp(amax / 6.0)
        byte = np.where(mant > 0.5, ex, ex - 1) + 127
    byte = np.clip(np.where(amax > 0, byte, 1), 1, 254)
    scaled = (w * np.exp2(127.0 - byte)[:, None, :]).reshape(k, n).astype(np.float32)
    by_word = np.ascontiguousarray(scaled.reshape(k // 512, 128, 4, n).transpose(0, 1, 3, 2))
    if fmt == "e4m3":
        words = by_word.astype(ml_dtypes.float8_e4m3fn).view(np.uint8)
    else:
        c = by_word.astype(ml_dtypes.float4_e2m1fn).view(np.uint8) & 0xF
        words = c[..., 0::2] | (c[..., 1::2] << 4)
    return np.ascontiguousarray(words), np.ascontiguousarray(byte.astype(np.uint8).reshape(k // 512, 16, n))


def unpack_weight(words, scales, fmt):
    g, p, n, _ = words.shape
    if fmt == "e4m3":
        vals = np.ascontiguousarray(words).view(ml_dtypes.float8_e4m3fn).astype(np.float64)
    else:
        nib = np.empty((g, p, n, 4), np.uint8)
        nib[..., 0::2] = words & 0xF
        nib[..., 1::2] = words >> 4
        vals = E2M1[nib]
    vals = vals * np.repeat(np.exp2(scales.astype(np.float64) - 127.0), 8, axis=1)[..., None]
    return vals.transpose(0, 1, 3, 2).reshape(g * 512, n)


BW, NW, WZ, WH, WW, C, H, HD = 2, 2, 2, 8, 8, 8192, 32, 24
N = WZ * WH * WW
F = 3 * H * HD
SCALE = HD ** -0.5
FMT = "e4m3"


def axis_rope(x, axis):
    d = x.shape[-1]
    L = x.shape[axis]
    inv_freq = 1.0 / (10000.0 ** (np.arange(0, d, 2) / d))
    ang = np.arange(L)[:, None] * inv_freq
    cos = np.concatenate([np.cos(ang), np.cos(ang)], -1)
    sin = np.concatenate([np.sin(ang), np.sin(ang)], -1)
    bshape = [1] * x.ndim
    bshape[axis] = L
    bshape[-1] = d
    cos = cos.reshape(bshape)
    sin = sin.reshape(bshape)
    x1, x2 = np.split(x, 2, axis=-1)
    rot = np.concatenate([-x2, x1], axis=-1)
    return x * cos + rot * sin


def rope3(x):
    d = x.shape[-1] // 3
    xz, xh, xw = x[..., :d], x[..., d:2 * d], x[..., 2 * d:]
    return np.concatenate([axis_rope(xz, 1), axis_rope(xh, 2), axis_rope(xw, 3)], -1)


def setup_inputs():
    s = mx_kscale(C)
    x = bf(np.random.standard_normal((BW, N, C)) * s)
    w = np.random.standard_normal((F, C)) / np.sqrt(C) / s
    words, scales = pack_weight(np.ascontiguousarray(w.T), FMT)
    qkv_b = bf(np.random.standard_normal(F) * 0.3)
    return {"x": x,
            "qkv_w_words": words,
            "qkv_w_scales": scales,
            "qkv_b": qkv_b}


def reference(x, qkv_w_words, qkv_w_scales, qkv_b):
    y = (mxq(f64(x), 2, "e4m3") @ unpack_weight(qkv_w_words, qkv_w_scales, FMT)) + f64(qkv_b)
    qkv = y.reshape(BW, N, 3, H, HD).transpose(2, 0, 3, 1, 4)
    q, k, v = qkv[0], qkv[1], qkv[2]
    q = rope3(q.reshape(-1, WZ, WH, WW, HD)).reshape(BW, H, N, HD)
    k = rope3(k.reshape(-1, WZ, WH, WW, HD)).reshape(BW, H, N, HD)
    return q * SCALE, k, np.ascontiguousarray(v)

@@ -1,0 +1,256 @@
+import math
+from contextlib import ExitStack
+
+import concourse.mybir as mybir
+from concourse.masks import make_identity
+
+F32 = mybir.dt.float32
+BF16 = mybir.dt.bfloat16
+I32 = mybir.dt.int32
+U32 = mybir.dt.uint32
+U8 = mybir.dt.uint8
+FP8X4 = mybir.dt.float8_e4m3fn_x4
+ALU = mybir.AluOpType
+ACT = mybir.ActivationFunctionType
+
+P = 128
+WINDOWS = 2
+K = 8192
+K_PASS = 512
+PASSES = K // K_PASS
+HEADS = 32
+HEAD_DIM = 24
+AXES = 3
+PAIRS = 4
+SECTION = HEADS * HEAD_DIM
+SECTIONS = 3
+COLUMNS = SECTIONS * SECTION
+BANK = 512
+PARTS = ((0, 512), (512, 256))
+LANES = 4
+SLOTS = PASSES // LANES
+X_CHUNK = LANES * K_PASS
+
+FLOPS = 2 * WINDOWS * P * K * COLUMNS
+
+
+def by_head(ap):
+    return ap.rearrange("p (h e) -> p h e", e=HEAD_DIM)
+
+
+def by_half(ap):
+    return ap.rearrange("p (h a s i) -> p h a s i", a=AXES, s=2, i=PAIRS)
+
+
+def spread_bias(nc, consts, psum, qkv_b):
+    bias_rows = consts.tile([P, COLUMNS], BF16)
+    nc.vector.memset(bias_rows[:], 0.0)
+    nc.scalar.dma_start(out=bias_rows[0:1, :], in_=qkv_b.rearrange("(o n) -> o n", o=1))
+    ones = consts.tile([P, P], BF16)
+    nc.vector.memset(ones[:], 1.0)
+    bias_all = consts.tile([P, COLUMNS], F32)
+    for first in range(0, COLUMNS, BANK):
+        width = min(BANK, COLUMNS - first)
+        summed = psum.tile([P, BANK], F32, tag="bank")
+        nc.tensor.matmul(
+            out=summed[:, :width],
+            lhsT=ones[:],
+            rhs=bias_rows[:, first : first + width],
+            start=True,
+            stop=True,
+        )
+        nc.vector.tensor_copy(out=bias_all[:, first : first + width], in_=summed[:, :width])
+    return bias_all
+
+
+def rotation_tables(nc, consts):
+    token = consts.tile([P, 1], I32)
+    nc.gpsimd.iota(out=token[:], pattern=[[0, 1]], base=0, channel_multiplier=1)
+    place_int = consts.tile([P, AXES], I32)
+    nc.vector.tensor_single_scalar(
+        out=place_int[:, 0:1], in_=token[:], scalar=6, op=ALU.logical_shift_right
+    )
+    nc.vector.tensor_scalar(
+        out=place_int[:, 1:2],
+        in0=token[:],
+        scalar1=3,
+        scalar2=7,
+        op0=ALU.logical_shift_right,
+        op1=ALU.bitwise_and,
+    )
+    nc.vector.tensor_single_scalar(
+        out=place_int[:, 2:3], in_=token[:], scalar=7, op=ALU.bitwise_and
+    )
+    place = consts.tile([P, AXES], F32)
+    nc.vector.tensor_copy(out=place[:], in_=place_int[:])
+
+    angles = consts.tile([P, 2, AXES, PAIRS], F32)
+    for pair in range(PAIRS):
+        nc.vector.tensor_single_scalar(
+            out=angles[:, 1, :, pair],
+            in_=place[:],
+            scalar=1.0 / (10000.0 ** (2 * pair / 8)),
+            op=ALU.mult,
+        )
+    nc.vector.tensor_single_scalar(
+        out=angles[:, 0], in_=angles[:, 1], scalar=math.pi / 2, op=ALU.add
+    )
+    turn = consts.tile([P, 2, AXES, PAIRS], F32)
+    nc.vector.tensor_scalar(
+        out=turn[:],
+        in0=angles[:],
+        scalar1=math.pi,
+        scalar2=2 * math.pi,
+        op0=ALU.is_gt,
+        op1=ALU.mult,
+    )
+    nc.vector.tensor_sub(out=angles[:], in0=angles[:], in1=turn[:])
+    cos_sin = consts.tile([P, 2, AXES, PAIRS], F32)
+    nc.scalar.activation(out=cos_sin[:], in_=angles[:], func=ACT.Sin)
+
+    cos_table = consts.tile([P, 2, AXES, 2, PAIRS], F32)
+    sin_table = consts.tile([P, 2, AXES, 2, PAIRS], F32)
+    for section, factor in enumerate((HEAD_DIM**-0.5, 1.0)):
+        nc.vector.tensor_single_scalar(
+            out=cos_table[:, section],
+            in_=cos_sin[:, 0].unsqueeze(2).to_broadcast([P, AXES, 2, PAIRS]),
+            scalar=factor,
+            op=ALU.mult,
+        )
+        nc.vector.tensor_single_scalar(
+            out=sin_table[:, section, :, 0, :], in_=cos_sin[:, 1], scalar=-factor, op=ALU.mult
+        )
+        nc.vector.tensor_single_scalar(
+            out=sin_table[:, section, :, 1, :], in_=cos_sin[:, 1], scalar=factor, op=ALU.mult
+        )
+    return cos_table, sin_table
+
+
+def rotate(nc, work, y, cos_row, sin_row):
+    straight = work.tile([P, SECTION], F32)
+    nc.vector.tensor_mul(
+        out=by_head(straight[:]),
+        in0=by_head(y[:]),
+        in1=cos_row.rearrange("p a s i -> p (a s i)")
+        .unsqueeze(1)
+        .to_broadcast([P, HEADS, HEAD_DIM]),
+    )
+    crossed = work.tile([P, SECTION], F32)
+    for half in range(2):
+        nc.vector.tensor_mul(
+            out=by_half(crossed[:])[:, :, :, half, :],
+            in0=by_half(y[:])[:, :, :, 1 - half, :],
+            in1=sin_row[:, :, half, :].unsqueeze(1).to_broadcast([P, HEADS, AXES, PAIRS]),
+        )
+    nc.vector.tensor_add(out=straight[:], in0=straight[:], in1=crossed[:])
+    return straight
+
+
+def tile_windowattention_pa_k_kernel(
+    tc, x, qkv_w_words, qkv_w_scales, qkv_b, out_0, out_1, out_2
+):
+    nc = tc.nc
+    outs = (out_0, out_1, out_2)
+    with ExitStack() as stack:
+        consts = stack.enter_context(tc.tile_pool(name="consts", bufs=1))
+        keep = stack.enter_context(tc.tile_pool(name="keep", bufs=1))
+        stage = stack.enter_context(tc.tile_pool(name="stage", bufs=4))
+        weights = stack.enter_context(tc.tile_pool(name="weights", bufs=6))
+        work = stack.enter_context(tc.tile_pool(name="work", bufs=2))
+        psum = stack.enter_context(tc.psum_pool(name="psum", bufs=8))
+
+        planes = keep.tile([P, SLOTS, COLUMNS], U8, align_bytes=64)
+        nc.vector.memset(planes[:].bitcast(I32), 0)
+
+        x_raw = [keep.tile([P, K], BF16, name="x_raw%d" % w) for w in range(WINDOWS)]
+        for first in range(0, K, X_CHUNK):
+            for w in range(WINDOWS):
+                nc.sync.dma_start(
+                    out=x_raw[w][:, first : first + X_CHUNK],
+                    in_=x[w, :, first : first + X_CHUNK],
+                )
+        for slot in range(SLOTS):
+            for quadrant in range(4):
+                nc.sync.dma_start(
+                    out=planes[32 * quadrant : 32 * quadrant + 4 * LANES, slot, :].bitcast(I32),
+                    in_=qkv_w_scales[
+                        LANES * slot : LANES * (slot + 1), 4 * quadrant : 4 * quadrant + 4, :
+                    ].bitcast(I32),
+                )
+
+        identity = consts.tile([P, P], F32)
+        make_identity(nc, identity[:])
+        bias_all = spread_bias(nc, consts, psum, qkv_b)
+        cos_table, sin_table = rotation_tables(nc, consts)
+
+        x_codes = keep.tile([P, PASSES, WINDOWS * P], U32, align_bytes=64)
+        x_scales = keep.tile([P, PASSES, WINDOWS * P], U8, align_bytes=64)
+        grouped = {}
+        for g in range(PASSES + 1):
+            if g < PASSES:
+                flipped = psum.tile([P, WINDOWS, 2, P], F32, tag="bank")
+                for w in range(WINDOWS):
+                    words = x_raw[w][:].bitcast(F32)
+                    for u in range(2):
+                        nc.tensor.transpose(
+                            out=flipped[:, w, u, :],
+                            in_=words[:, 256 * g + u : 256 * (g + 1) : 2],
+                            identity=identity[:],
+                        )
+                grouped[g] = stage.tile([P, WINDOWS * P * 4], BF16, align_bytes=64, name="grouped")
+                nc.scalar.copy(
+                    out=grouped[g][:].bitcast(F32).rearrange("p (w r u) -> p w r u", w=WINDOWS, u=2),
+                    in_=flipped[:].rearrange("p w u r -> p w r u"),
+                )
+            if g > 0:
+                nc.vector.quantize_mx(
+                    out=x_codes[:, g - 1, :].bitcast(FP8X4),
+                    scales=x_scales[:, g - 1, :],
+                    in_=grouped[g - 1][:],
+                )
+
+        w_by_partition = qkv_w_words.rearrange("g p n t -> p g (n t)")
+        for section in range(SECTIONS):
+            column0 = section * SECTION
+            sums = [
+                [psum.tile([P, BANK], F32, tag="bank", name="sums") for part in PARTS]
+                for w in range(WINDOWS)
+            ]
+            for slot in range(SLOTS):
+                w_words = weights.tile([P, LANES, SECTION], U32, align_bytes=64)
+                nc.sync.dma_start(
+                    out=w_words[:].bitcast(I32),
+                    in_=w_by_partition[
+                        :, LANES * slot : LANES * (slot + 1), 4 * column0 : 4 * (column0 + SECTION)
+                    ].bitcast(I32),
+                )
+                for lane in range(LANES):
+                    g = LANES * slot + lane
+                    for w in range(WINDOWS):
+                        tokens = slice(w * P, (w + 1) * P)
+                        for (first, width), bank in zip(PARTS, sums[w]):
+                            nc.tensor.matmul_mx(
+                                out=bank[:, :width],
+                                lhsT=x_codes[:, g, tokens].bitcast(FP8X4),
+                                lhsT_scale=x_scales[:, g, tokens],
+                                rhs=w_words[:, lane, first : first + width].bitcast(FP8X4),
+                                rhs_scale=planes[
+                                    4 * lane : P, slot, column0 + first : column0 + first + width
+                                ],
+                                start=(g == 0),
+                                stop=(g == PASSES - 1),
+                            )
+
+            for w in range(WINDOWS):
+                y = work.tile([P, SECTION], F32)
+                for (first, width), bank in zip(PARTS, sums[w]):
+                    nc.vector.tensor_add(
+                        out=y[:, first : first + width],
+                        in0=bank[:, :width],
+                        in1=bias_all[:, column0 + first : column0 + first + width],
+                    )
+                if section < 2:
+                    y = rotate(nc, work, y, cos_table[:, section], sin_table[:, section])
+                nc.scalar.dma_start(
+                    out=outs[section][w].rearrange("h n e -> n h e"), in_=by_head(y[:])
+                )

@@ -21,37 +21,39 @@ PASSES = K // K_PASS
 HEADS = 32
 HEAD_DIM = 24
 AXES = 3
-PAIRS = 4
+GROUP = HEAD_DIM // AXES
+PAIRS = GROUP // 2
 SECTION = HEADS * HEAD_DIM
 SECTIONS = 3
+ROTATED = 2
 COLUMNS = SECTIONS * SECTION
 BANK = 512
 PARTS = ((0, 512), (512, 256))
 LANES = 4
 SLOTS = PASSES // LANES
 X_CHUNK = LANES * K_PASS
+ROWS = WINDOWS * HEADS
+ROW0 = (P - ROWS) // 2
+PER_BANK = BANK // P
+FLIP_AFTER_SLOTS = 3
 
 FLOPS = 2 * WINDOWS * P * K * COLUMNS
 
 
-def by_head(ap):
-    return ap.rearrange("p (h e) -> p h e", e=HEAD_DIM)
-
-
-def by_half(ap):
-    return ap.rearrange("p (h a s i) -> p h a s i", a=AXES, s=2, i=PAIRS)
-
-
-def spread_bias(nc, consts, psum, qkv_b):
+def load_bias(nc, consts, qkv_b):
     bias_rows = consts.tile([P, COLUMNS], BF16)
     nc.vector.memset(bias_rows[:], 0.0)
     nc.scalar.dma_start(out=bias_rows[0:1, :], in_=qkv_b.rearrange("(o n) -> o n", o=1))
+    return bias_rows
+
+
+def spread_bias(nc, consts, psum, bias_rows):
     ones = consts.tile([P, P], BF16)
     nc.vector.memset(ones[:], 1.0)
     bias_all = consts.tile([P, COLUMNS], F32)
     for first in range(0, COLUMNS, BANK):
         width = min(BANK, COLUMNS - first)
-        summed = psum.tile([P, BANK], F32, tag="bank")
+        summed = psum.tile([P, BANK], F32, tag="bank_b")
         nc.tensor.matmul(
             out=summed[:, :width],
             lhsT=ones[:],
@@ -60,7 +62,12 @@ def spread_bias(nc, consts, psum, qkv_b):
             stop=True,
         )
         nc.vector.tensor_copy(out=bias_all[:, first : first + width], in_=summed[:, :width])
-    return bias_all
+    bias_by_feature = consts.tile([P, SECTIONS, HEAD_DIM, HEADS], F32)
+    nc.vector.tensor_copy(
+        out=bias_by_feature[:],
+        in_=bias_all[:].rearrange("p (s h e) -> p s e h", s=SECTIONS, e=HEAD_DIM),
+    )
+    return bias_by_feature
 
 
 def rotation_tables(nc, consts):
@@ -126,24 +133,59 @@ def rotation_tables(nc, consts):
     return cos_table, sin_table
 
 
-def rotate(nc, work, y, cos_row, sin_row):
-    straight = work.tile([P, SECTION], F32)
+def add_bias(nc, target, sums, bias_section):
+    for axis in range(AXES):
+        features = slice(GROUP * axis, GROUP * (axis + 1))
+        for w in range(WINDOWS):
+            for (first, width), bank in zip(PARTS, sums[w]):
+                groups = bank[:, :width].rearrange("p (g f) -> p g f", f=GROUP)
+                start = (axis - first // GROUP) % AXES
+                head0 = (first // GROUP + start) // AXES
+                heads = len(range(start, width // GROUP, AXES))
+                nc.vector.tensor_add(
+                    out=target[:, features, w * HEADS + head0 : w * HEADS + head0 + heads],
+                    in0=groups[:, start : width // GROUP : AXES, :].rearrange("p h f -> p f h"),
+                    in1=bias_section[:, features, head0 : head0 + heads],
+                )
+
+
+def rotate(nc, work, target, y, cos_rows, sin_rows):
+    straight = work.tile([P, HEAD_DIM, ROWS], F32)
     nc.vector.tensor_mul(
-        out=by_head(straight[:]),
-        in0=by_head(y[:]),
-        in1=cos_row.rearrange("p a s i -> p (a s i)")
-        .unsqueeze(1)
-        .to_broadcast([P, HEADS, HEAD_DIM]),
+        out=straight[:],
+        in0=y[:],
+        in1=cos_rows.rearrange("p a s i -> p (a s i)")
+        .unsqueeze(2)
+        .to_broadcast([P, HEAD_DIM, ROWS]),
     )
-    crossed = work.tile([P, SECTION], F32)
+    crossed = work.tile([P, AXES, 2, PAIRS, ROWS], F32)
+    halves = y[:].rearrange("p (a s i) c -> p a s i c", a=AXES, s=2)
     for half in range(2):
         nc.vector.tensor_mul(
-            out=by_half(crossed[:])[:, :, :, half, :],
-            in0=by_half(y[:])[:, :, :, 1 - half, :],
-            in1=sin_row[:, :, half, :].unsqueeze(1).to_broadcast([P, HEADS, AXES, PAIRS]),
+            out=crossed[:, :, half],
+            in0=halves[:, :, 1 - half],
+            in1=sin_rows[:, :, half, :].unsqueeze(3).to_broadcast([P, AXES, PAIRS, ROWS]),
         )
-    nc.vector.tensor_add(out=straight[:], in0=straight[:], in1=crossed[:])
-    return straight
+    nc.vector.tensor_add(
+        out=target, in0=straight[:], in1=crossed[:].rearrange("p a s i c -> p (a s i) c")
+    )
+
+
+def flip_and_store(nc, psum, bank_tag, by_feature, by_row, identity, out):
+    for first in range(0, HEAD_DIM, PER_BANK):
+        flipped = psum.tile([P, PER_BANK, P], F32, tag=bank_tag)
+        for e in range(PER_BANK):
+            nc.tensor.transpose(
+                out=flipped[:, e, :], in_=by_feature[:, first + e, :], identity=identity[:]
+            )
+        nc.scalar.copy(
+            out=by_row[:, :, first : first + PER_BANK],
+            in_=flipped[:].rearrange("c e n -> c n e"),
+        )
+    nc.scalar.dma_start(
+        out=out.rearrange("w h n e -> (w h) (n e)"),
+        in_=by_row[ROW0 : ROW0 + ROWS].rearrange("c n e -> c (n e)"),
+    )
 
 
 def tile_windowattention_pa_k_kernel(
@@ -152,15 +194,18 @@ def tile_windowattention_pa_k_kernel(
     nc = tc.nc
     outs = (out_0, out_1, out_2)
     with ExitStack() as stack:
+        stack.enter_context(tc.manual_schedule())
         consts = stack.enter_context(tc.tile_pool(name="consts", bufs=1))
         keep = stack.enter_context(tc.tile_pool(name="keep", bufs=1))
         stage = stack.enter_context(tc.tile_pool(name="stage", bufs=4))
         weights = stack.enter_context(tc.tile_pool(name="weights", bufs=6))
-        work = stack.enter_context(tc.tile_pool(name="work", bufs=2))
-        psum = stack.enter_context(tc.psum_pool(name="psum", bufs=8))
+        work = stack.enter_context(tc.tile_pool(name="work", bufs=1))
+        psum = stack.enter_context(tc.psum_pool(name="psum", bufs=4))
+        bank_tags = ("bank_a", "bank_b")
 
         planes = keep.tile([P, SLOTS, COLUMNS], U8, align_bytes=64)
         nc.vector.memset(planes[:].bitcast(I32), 0)
+        bias_rows = load_bias(nc, consts, qkv_b)
 
         x_raw = [keep.tile([P, K], BF16, name="x_raw%d" % w) for w in range(WINDOWS)]
         for first in range(0, K, X_CHUNK):
@@ -178,45 +223,50 @@ def tile_windowattention_pa_k_kernel(
                     ].bitcast(I32),
                 )
 
+        cos_table, sin_table = rotation_tables(nc, consts)
         identity = consts.tile([P, P], F32)
         make_identity(nc, identity[:])
-        bias_all = spread_bias(nc, consts, psum, qkv_b)
-        cos_table, sin_table = rotation_tables(nc, consts)
 
         x_codes = keep.tile([P, PASSES, WINDOWS * P], U32, align_bytes=64)
         x_scales = keep.tile([P, PASSES, WINDOWS * P], U8, align_bytes=64)
-        grouped = {}
-        for g in range(PASSES + 1):
-            if g < PASSES:
-                flipped = psum.tile([P, WINDOWS, 2, P], F32, tag="bank")
-                for w in range(WINDOWS):
-                    words = x_raw[w][:].bitcast(F32)
-                    for u in range(2):
-                        nc.tensor.transpose(
-                            out=flipped[:, w, u, :],
-                            in_=words[:, 256 * g + u : 256 * (g + 1) : 2],
-                            identity=identity[:],
-                        )
-                grouped[g] = stage.tile([P, WINDOWS * P * 4], BF16, align_bytes=64, name="grouped")
-                nc.scalar.copy(
-                    out=grouped[g][:].bitcast(F32).rearrange("p (w r u) -> p w r u", w=WINDOWS, u=2),
-                    in_=flipped[:].rearrange("p w u r -> p w r u"),
-                )
-            if g > 0:
-                nc.vector.quantize_mx(
-                    out=x_codes[:, g - 1, :].bitcast(FP8X4),
-                    scales=x_scales[:, g - 1, :],
-                    in_=grouped[g - 1][:],
-                )
+        for g in range(PASSES):
+            flipped = psum.tile([P, WINDOWS, 2, P], F32, tag="bank_b")
+            for w in range(WINDOWS):
+                words = x_raw[w][:].bitcast(F32)
+                for u in range(2):
+                    nc.tensor.transpose(
+                        out=flipped[:, w, u, :],
+                        in_=words[:, 256 * g + u : 256 * (g + 1) : 2],
+                        identity=identity[:],
+                    )
+            grouped = stage.tile([P, WINDOWS * P * 4], BF16, align_bytes=64)
+            nc.scalar.copy(
+                out=grouped[:].bitcast(F32).rearrange("p (w r u) -> p w r u", w=WINDOWS, u=2),
+                in_=flipped[:].rearrange("p w u r -> p w r u"),
+            )
+            nc.vector.quantize_mx(
+                out=x_codes[:, g, :].bitcast(FP8X4), scales=x_scales[:, g, :], in_=grouped[:]
+            )
+
+        bias_by_feature = spread_bias(nc, consts, psum, bias_rows)
+        by_feature = keep.tile([P, HEAD_DIM, P], F32)
+        nc.vector.memset(by_feature[:], 0.0)
+        by_row = keep.tile([P, P, HEAD_DIM], F32)
 
         w_by_partition = qkv_w_words.rearrange("g p n t -> p g (n t)")
+        rows = by_feature[:, :, ROW0 : ROW0 + ROWS]
         for section in range(SECTIONS):
             column0 = section * SECTION
             sums = [
-                [psum.tile([P, BANK], F32, tag="bank", name="sums") for part in PARTS]
+                [psum.tile([P, BANK], F32, tag=bank_tags[section % 2], name="sums") for part in PARTS]
                 for w in range(WINDOWS)
             ]
             for slot in range(SLOTS):
+                if section > 0 and slot == FLIP_AFTER_SLOTS:
+                    flip_and_store(
+                        nc, psum, bank_tags[(section - 1) % 2], by_feature, by_row, identity,
+                        outs[section - 1],
+                    )
                 w_words = weights.tile([P, LANES, SECTION], U32, align_bytes=64)
                 nc.sync.dma_start(
                     out=w_words[:].bitcast(I32),
@@ -241,16 +291,13 @@ def tile_windowattention_pa_k_kernel(
                                 stop=(g == PASSES - 1),
                             )
 
-            for w in range(WINDOWS):
-                y = work.tile([P, SECTION], F32)
-                for (first, width), bank in zip(PARTS, sums[w]):
-                    nc.vector.tensor_add(
-                        out=y[:, first : first + width],
-                        in0=bank[:, :width],
-                        in1=bias_all[:, column0 + first : column0 + first + width],
-                    )
-                if section < 2:
-                    y = rotate(nc, work, y, cos_table[:, section], sin_table[:, section])
-                nc.scalar.dma_start(
-                    out=outs[section][w].rearrange("h n e -> n h e"), in_=by_head(y[:])
-                )
+            if section < ROTATED:
+                y = work.tile([P, HEAD_DIM, ROWS], F32)
+                add_bias(nc, y[:], sums, bias_by_feature[:, section])
+                rotate(nc, work, rows, y, cos_table[:, section], sin_table[:, section])
+            else:
+                add_bias(nc, rows, sums, bias_by_feature[:, section])
+        flip_and_store(
+            nc, psum, bank_tags[(SECTIONS - 1) % 2], by_feature, by_row, identity,
+            outs[SECTIONS - 1],
+        )

@@ -25,24 +25,31 @@ GROUP = HEAD_DIM // AXES
 PAIRS = GROUP // 2
 SECTION = HEADS * HEAD_DIM
 SECTIONS = 3
-ROTATED = 2
 COLUMNS = SECTIONS * SECTION
 BANK = 512
-PARTS = ((0, 512), (512, 256))
+BANKS = 8
 LANES = 4
 SLOTS = PASSES // LANES
-X_CHUNK = LANES * K_PASS
 ROWS = WINDOWS * HEADS
-ROW0 = (P - ROWS) // 2
 PER_BANK = BANK // P
-FLIP_AFTER_SLOTS = 3
+
+QK_COLUMNS = 2 * SECTION
+QK_PARTS = QK_COLUMNS // BANK
+V_PARTS = ((0, 512), (512, 256))
+X_BANKS = (0, 1)
+QK_BANKS = ((2, 3, 4), (5, 6, 7))
+V_BANKS = ((0, 2), (1, 5))
+FLIP_BANKS = (3, 6, 4, 7)
+W_PASSES = 2
+ROW0 = 32
+BIAS_FEATURES = 12
 
 FLOPS = 2 * WINDOWS * P * K * COLUMNS
 
 
 def load_bias(nc, consts, qkv_b):
     bias_rows = consts.tile([P, COLUMNS], BF16)
-    nc.vector.memset(bias_rows[:], 0.0)
+    nc.vector.memset(bias_rows[:].bitcast(I32), 0)
     nc.scalar.dma_start(out=bias_rows[0:1, :], in_=qkv_b.rearrange("(o n) -> o n", o=1))
     return bias_rows
 
@@ -50,24 +57,30 @@ def load_bias(nc, consts, qkv_b):
 def spread_bias(nc, consts, psum, bias_rows):
     ones = consts.tile([P, P], BF16)
     nc.vector.memset(ones[:], 1.0)
-    bias_all = consts.tile([P, COLUMNS], F32)
-    for first in range(0, COLUMNS, BANK):
-        width = min(BANK, COLUMNS - first)
-        summed = psum.tile([P, BANK], F32, tag="bank_b")
-        nc.tensor.matmul(
-            out=summed[:, :width],
-            lhsT=ones[:],
-            rhs=bias_rows[:, first : first + width],
-            start=True,
-            stop=True,
+    bias_all = consts.tile([P, SECTIONS, HEAD_DIM, HEADS], F32)
+    block = 0
+    for section in range(SECTIONS):
+        by_feature = bias_rows[:, section * SECTION : (section + 1) * SECTION].rearrange(
+            "p (h e) -> p e h", e=HEAD_DIM
         )
-        nc.vector.tensor_copy(out=bias_all[:, first : first + width], in_=summed[:, :width])
-    bias_by_feature = consts.tile([P, SECTIONS, HEAD_DIM, HEADS], F32)
-    nc.vector.tensor_copy(
-        out=bias_by_feature[:],
-        in_=bias_all[:].rearrange("p (s h e) -> p s e h", s=SECTIONS, e=HEAD_DIM),
-    )
-    return bias_by_feature
+        for first in range(0, HEAD_DIM, BIAS_FEATURES):
+            summed = psum.tile([P, BANK], F32, tag="bank%d" % (2 + block), name="summed")
+            width = BIAS_FEATURES * HEADS
+            nc.tensor.matmul(
+                out=summed[:, :width],
+                lhsT=ones[:],
+                rhs=by_feature[:, first : first + BIAS_FEATURES, :],
+                start=True,
+                stop=True,
+            )
+            nc.vector.tensor_copy(
+                out=bias_all[:, section, first : first + BIAS_FEATURES, :].rearrange(
+                    "p e h -> p (e h)"
+                ),
+                in_=summed[:, :width],
+            )
+            block += 1
+    return bias_all
 
 
 def rotation_tables(nc, consts):
@@ -133,33 +146,35 @@ def rotation_tables(nc, consts):
     return cos_table, sin_table
 
 
-def add_bias(nc, target, sums, bias_section):
-    for axis in range(AXES):
-        features = slice(GROUP * axis, GROUP * (axis + 1))
-        for w in range(WINDOWS):
-            for (first, width), bank in zip(PARTS, sums[w]):
-                groups = bank[:, :width].rearrange("p (g f) -> p g f", f=GROUP)
-                start = (axis - first // GROUP) % AXES
-                head0 = (first // GROUP + start) // AXES
-                heads = len(range(start, width // GROUP, AXES))
-                nc.vector.tensor_add(
-                    out=target[:, features, w * HEADS + head0 : w * HEADS + head0 + heads],
-                    in0=groups[:, start : width // GROUP : AXES, :].rearrange("p h f -> p f h"),
-                    in1=bias_section[:, features, head0 : head0 + heads],
-                )
+def add_bias_axis(nc, axis, target, pieces, bias_section):
+    features = slice(GROUP * axis, GROUP * (axis + 1))
+    for w in range(WINDOWS):
+        for first, sums in pieces[w]:
+            width = sums.shape[1]
+            groups = sums.rearrange("p (g f) -> p g f", f=GROUP)
+            start = (axis - first // GROUP) % AXES
+            head0 = (first // GROUP + start) // AXES
+            heads = len(range(start, width // GROUP, AXES))
+            nc.vector.tensor_add(
+                out=target[:, features, w, head0 : head0 + heads],
+                in0=groups[:, start : width // GROUP : AXES, :].rearrange("p h f -> p f h"),
+                in1=bias_section[:, features, head0 : head0 + heads],
+            )
 
 
 def rotate(nc, work, target, y, cos_rows, sin_rows):
-    straight = work.tile([P, HEAD_DIM, ROWS], F32)
-    nc.vector.tensor_mul(
-        out=straight[:],
-        in0=y[:],
-        in1=cos_rows.rearrange("p a s i -> p (a s i)")
-        .unsqueeze(2)
-        .to_broadcast([P, HEAD_DIM, ROWS]),
-    )
-    crossed = work.tile([P, AXES, 2, PAIRS, ROWS], F32)
+    straight = work.tile([P, HEAD_DIM, ROWS], F32, name="straight")
+    crossed = work.tile([P, AXES, 2, PAIRS, ROWS], F32, name="crossed")
     halves = y[:].rearrange("p (a s i) c -> p a s i c", a=AXES, s=2)
+    straight_halves = straight[:].rearrange("p (a s i) c -> p a s i c", a=AXES, s=2)
+    for axis in range(AXES):
+        for pair in range(PAIRS):
+            nc.scalar.activation(
+                out=straight_halves[:, axis, :, pair, :],
+                in_=halves[:, axis, :, pair, :],
+                func=ACT.Copy,
+                scale=cos_rows[:, axis, 0, pair : pair + 1],
+            )
     for half in range(2):
         nc.vector.tensor_mul(
             out=crossed[:, :, half],
@@ -167,137 +182,227 @@ def rotate(nc, work, target, y, cos_rows, sin_rows):
             in1=sin_rows[:, :, half, :].unsqueeze(3).to_broadcast([P, AXES, PAIRS, ROWS]),
         )
     nc.vector.tensor_add(
-        out=target, in0=straight[:], in1=crossed[:].rearrange("p a s i c -> p (a s i) c")
+        out=target,
+        in0=straight[:].rearrange("p e (w h) -> p e w h", w=WINDOWS),
+        in1=crossed[:].rearrange("p a s i (w h) -> p (a s i) w h", w=WINDOWS),
     )
 
 
-def flip_and_store(nc, psum, bank_tag, by_feature, by_row, identity, out):
-    for first in range(0, HEAD_DIM, PER_BANK):
-        flipped = psum.tile([P, PER_BANK, P], F32, tag=bank_tag)
+def flip(nc, psum, by_feature, by_row, identity, first_feature, features, copies):
+    for i, first in enumerate(range(first_feature, first_feature + features, PER_BANK)):
+        bank = FLIP_BANKS[(first // PER_BANK) % len(FLIP_BANKS)]
+        flipped = psum.tile([P, PER_BANK, P], F32, tag="bank%d" % bank, name="flipped")
         for e in range(PER_BANK):
             nc.tensor.transpose(
                 out=flipped[:, e, :], in_=by_feature[:, first + e, :], identity=identity[:]
             )
-        nc.scalar.copy(
+        copies[i](
             out=by_row[:, :, first : first + PER_BANK],
             in_=flipped[:].rearrange("c e n -> c n e"),
         )
-    nc.scalar.dma_start(
-        out=out.rearrange("w h n e -> (w h) (n e)"),
-        in_=by_row[ROW0 : ROW0 + ROWS].rearrange("c n e -> c (n e)"),
-    )
 
 
 def tile_windowattention_pa_k_kernel(
     tc, x, qkv_w_words, qkv_w_scales, qkv_b, out_0, out_1, out_2
 ):
     nc = tc.nc
-    outs = (out_0, out_1, out_2)
     with ExitStack() as stack:
         stack.enter_context(tc.manual_schedule())
         consts = stack.enter_context(tc.tile_pool(name="consts", bufs=1))
         keep = stack.enter_context(tc.tile_pool(name="keep", bufs=1))
+        x_pool = stack.enter_context(tc.tile_pool(name="x_pool", bufs=3))
         stage = stack.enter_context(tc.tile_pool(name="stage", bufs=4))
-        weights = stack.enter_context(tc.tile_pool(name="weights", bufs=6))
+        weights = stack.enter_context(tc.tile_pool(name="weights", bufs=7))
         work = stack.enter_context(tc.tile_pool(name="work", bufs=1))
-        psum = stack.enter_context(tc.psum_pool(name="psum", bufs=4))
-        bank_tags = ("bank_a", "bank_b")
+        psum = stack.enter_context(tc.psum_pool(name="psum", bufs=1))
 
-        planes = keep.tile([P, SLOTS, COLUMNS], U8, align_bytes=64)
-        nc.vector.memset(planes[:].bitcast(I32), 0)
+        def bank(i):
+            return psum.tile([P, BANK], F32, tag="bank%d" % i, name="bank")
+
+        identity = consts.tile([P, P], F32)
+        make_identity(nc, identity[:])
+
+        planes = [
+            keep.tile([P, COLUMNS], U8, align_bytes=64, name="planes%d" % slot)
+            for slot in range(SLOTS)
+        ]
         bias_rows = load_bias(nc, consts, qkv_b)
+        for slot in range(SLOTS):
+            nc.vector.memset(planes[slot][:].bitcast(I32), 0)
+        w_by_partition = qkv_w_words.rearrange("g p n t -> p g (n t)")
 
-        x_raw = [keep.tile([P, K], BF16, name="x_raw%d" % w) for w in range(WINDOWS)]
-        for first in range(0, K, X_CHUNK):
+        x_words = {}
+
+        def load_x(pass0, passes):
+            raw = x_pool.tile([P, WINDOWS, passes * K_PASS], BF16, tag="x", name="x_raw")
             for w in range(WINDOWS):
                 nc.sync.dma_start(
-                    out=x_raw[w][:, first : first + X_CHUNK],
-                    in_=x[w, :, first : first + X_CHUNK],
+                    out=raw[:, w, :], in_=x[w, :, pass0 * K_PASS : (pass0 + passes) * K_PASS]
                 )
-        for slot in range(SLOTS):
+            for i in range(passes):
+                x_words[pass0 + i] = raw[:, :, i * K_PASS : (i + 1) * K_PASS]
+
+        def load_scales(slot):
             for quadrant in range(4):
                 nc.sync.dma_start(
-                    out=planes[32 * quadrant : 32 * quadrant + 4 * LANES, slot, :].bitcast(I32),
+                    out=planes[slot][32 * quadrant : 32 * quadrant + 4 * LANES, :].bitcast(I32),
                     in_=qkv_w_scales[
                         LANES * slot : LANES * (slot + 1), 4 * quadrant : 4 * quadrant + 4, :
                     ].bitcast(I32),
                 )
 
-        cos_table, sin_table = rotation_tables(nc, consts)
-        identity = consts.tile([P, P], F32)
-        make_identity(nc, identity[:])
+        def load_w(pass0, passes, column0, columns):
+            words = weights.tile([P, passes, columns], U32, align_bytes=64, tag="w", name="w_words")
+            nc.sync.dma_start(
+                out=words[:].bitcast(I32),
+                in_=w_by_partition[
+                    :, pass0 : pass0 + passes, 4 * column0 : 4 * (column0 + columns)
+                ].bitcast(I32),
+            )
+            return words
 
         x_codes = keep.tile([P, PASSES, WINDOWS * P], U32, align_bytes=64)
         x_scales = keep.tile([P, PASSES, WINDOWS * P], U8, align_bytes=64)
-        for g in range(PASSES):
-            flipped = psum.tile([P, WINDOWS, 2, P], F32, tag="bank_b")
+
+        def quantise_pass(g):
+            flipped = bank(X_BANKS[g % 2])[:].rearrange("p (w u r) -> p w u r", w=WINDOWS, u=2)
             for w in range(WINDOWS):
-                words = x_raw[w][:].bitcast(F32)
+                words = x_words[g][:, w, :].bitcast(F32)
                 for u in range(2):
                     nc.tensor.transpose(
                         out=flipped[:, w, u, :],
-                        in_=words[:, 256 * g + u : 256 * (g + 1) : 2],
+                        in_=words[:, u::2],
                         identity=identity[:],
                     )
-            grouped = stage.tile([P, WINDOWS * P * 4], BF16, align_bytes=64)
+            grouped = stage.tile([P, WINDOWS * P * 4], BF16, align_bytes=64, name="grouped")
             nc.scalar.copy(
                 out=grouped[:].bitcast(F32).rearrange("p (w r u) -> p w r u", w=WINDOWS, u=2),
-                in_=flipped[:].rearrange("p w u r -> p w r u"),
+                in_=flipped.rearrange("p w u r -> p w r u"),
             )
             nc.vector.quantize_mx(
                 out=x_codes[:, g, :].bitcast(FP8X4), scales=x_scales[:, g, :], in_=grouped[:]
             )
 
-        bias_by_feature = spread_bias(nc, consts, psum, bias_rows)
-        by_feature = keep.tile([P, HEAD_DIM, P], F32)
-        nc.vector.memset(by_feature[:], 0.0)
-        by_row = keep.tile([P, P, HEAD_DIM], F32)
+        def multiply(g, w, target, words, column):
+            width = target.shape[1]
+            tokens = slice(w * P, (w + 1) * P)
+            slot, lane = divmod(g, LANES)
+            nc.tensor.matmul_mx(
+                out=target,
+                lhsT=x_codes[:, g, tokens].bitcast(FP8X4),
+                lhsT_scale=x_scales[:, g, tokens],
+                rhs=words.bitcast(FP8X4),
+                rhs_scale=planes[slot][4 * lane : P, column : column + width],
+                start=(g == 0),
+                stop=(g == PASSES - 1),
+            )
 
-        w_by_partition = qkv_w_words.rearrange("g p n t -> p g (n t)")
-        rows = by_feature[:, :, ROW0 : ROW0 + ROWS]
-        for section in range(SECTIONS):
-            column0 = section * SECTION
-            sums = [
-                [psum.tile([P, BANK], F32, tag=bank_tags[section % 2], name="sums") for part in PARTS]
+        qk_by_feature = keep.tile([P, HEAD_DIM, P], F32)
+        qk_by_row = keep.tile([P, P, HEAD_DIM], F32)
+        v_by_feature = keep.tile([P, HEAD_DIM, P], F32)
+        v_by_row = keep.tile([P, P, HEAD_DIM], F32)
+
+        load_x(0, W_PASSES)
+        load_scales(0)
+        w_next = load_w(0, W_PASSES, 0, QK_COLUMNS)
+        load_x(W_PASSES, W_PASSES)
+        bias_all = spread_bias(nc, consts, psum, bias_rows)
+        for g in range(W_PASSES):
+            quantise_pass(g)
+        qk_sums = [[None] * QK_PARTS for w in range(WINDOWS)]
+        for pass0 in range(0, PASSES, W_PASSES):
+            words = w_next
+            after = pass0 + W_PASSES
+            if after < PASSES:
+                if after % LANES == 0:
+                    load_x(after, LANES)
+                    load_scales(after // LANES)
+                w_next = load_w(after, W_PASSES, 0, QK_COLUMNS)
+                for g in range(after, after + W_PASSES):
+                    quantise_pass(g)
+            if pass0 == 0:
+                for w in range(WINDOWS):
+                    for part in range(QK_PARTS):
+                        qk_sums[w][part] = bank(QK_BANKS[w][part])
+                cos_table, sin_table = rotation_tables(nc, consts)
+                nc.vector.memset(v_by_feature[:], 0.0)
+            steps = [
+                (i, w, part)
+                for i in range(W_PASSES)
                 for w in range(WINDOWS)
+                for part in range(QK_PARTS)
             ]
-            for slot in range(SLOTS):
-                if section > 0 and slot == FLIP_AFTER_SLOTS:
-                    flip_and_store(
-                        nc, psum, bank_tags[(section - 1) % 2], by_feature, by_row, identity,
-                        outs[section - 1],
-                    )
-                w_words = weights.tile([P, LANES, SECTION], U32, align_bytes=64)
-                nc.sync.dma_start(
-                    out=w_words[:].bitcast(I32),
-                    in_=w_by_partition[
-                        :, LANES * slot : LANES * (slot + 1), 4 * column0 : 4 * (column0 + SECTION)
-                    ].bitcast(I32),
+            if after == PASSES:
+                steps = sorted(steps, key=lambda step: step[2])
+            for i, w, part in steps:
+                multiply(
+                    pass0 + i,
+                    w,
+                    qk_sums[w][part][:],
+                    words[:, i, part * BANK : (part + 1) * BANK],
+                    part * BANK,
                 )
-                for lane in range(LANES):
-                    g = LANES * slot + lane
-                    for w in range(WINDOWS):
-                        tokens = slice(w * P, (w + 1) * P)
-                        for (first, width), bank in zip(PARTS, sums[w]):
-                            nc.tensor.matmul_mx(
-                                out=bank[:, :width],
-                                lhsT=x_codes[:, g, tokens].bitcast(FP8X4),
-                                lhsT_scale=x_scales[:, g, tokens],
-                                rhs=w_words[:, lane, first : first + width].bitcast(FP8X4),
-                                rhs_scale=planes[
-                                    4 * lane : P, slot, column0 + first : column0 + first + width
-                                ],
-                                start=(g == 0),
-                                stop=(g == PASSES - 1),
-                            )
 
-            if section < ROTATED:
-                y = work.tile([P, HEAD_DIM, ROWS], F32)
-                add_bias(nc, y[:], sums, bias_by_feature[:, section])
-                rotate(nc, work, rows, y, cos_table[:, section], sin_table[:, section])
-            else:
-                add_bias(nc, rows, sums, bias_by_feature[:, section])
-        flip_and_store(
-            nc, psum, bank_tags[(SECTIONS - 1) % 2], by_feature, by_row, identity,
-            outs[SECTIONS - 1],
+        half_bank = BANK // 2
+        q_pieces = [
+            [(0, qk_sums[w][0][:]), (BANK, qk_sums[w][1][:, :half_bank])] for w in range(WINDOWS)
+        ]
+        k_pieces = [
+            [(0, qk_sums[w][1][:, half_bank:]), (half_bank, qk_sums[w][2][:])]
+            for w in range(WINDOWS)
+        ]
+        q_rows = qk_by_feature[:, :, ROW0 : ROW0 + ROWS].rearrange(
+            "p e (w h) -> p e w h", w=WINDOWS
+        )
+        k_rows = qk_by_feature[:].rearrange("p e (w h) -> p e w h", h=HEADS)[:, :, 0:4:3, :]
+        for section, pieces, rows in ((0, q_pieces, q_rows), (1, k_pieces, k_rows)):
+            y = work.tile([P, HEAD_DIM, ROWS], F32, name="y")
+            y_by_window = y[:].rearrange("p e (w h) -> p e w h", w=WINDOWS)
+            for axis in range(AXES):
+                add_bias_axis(nc, axis, y_by_window, pieces, bias_all[:, section])
+            rotate(nc, work, rows, y, cos_table[:, section], sin_table[:, section])
+
+        v_sums = [[bank(V_BANKS[w][0]), None] for w in range(WINDOWS)]
+        for slot in range(SLOTS):
+            words = load_w(slot * LANES, LANES, QK_COLUMNS, SECTION)
+            for part, (first, width) in enumerate(V_PARTS):
+                if slot == 0 and part == 1:
+                    for w in range(WINDOWS):
+                        v_sums[w][1] = bank(V_BANKS[w][1])
+                if slot == SLOTS - 1 and part == 1:
+                    flip(
+                        nc, psum, qk_by_feature, qk_by_row, identity, 0, HEAD_DIM,
+                        [nc.scalar.copy] * 6,
+                    )
+                for lane in range(LANES):
+                    for w in range(WINDOWS):
+                        multiply(
+                            slot * LANES + lane,
+                            w,
+                            v_sums[w][part][:, :width],
+                            words[:, lane, first : first + width],
+                            QK_COLUMNS + first,
+                        )
+        nc.sync.dma_start(
+            out=out_0.rearrange("w h n e -> (w h) (n e)"),
+            in_=qk_by_row[ROW0 : ROW0 + ROWS].rearrange("c n e -> c (n e)"),
+        )
+        for w, row in ((0, 0), (1, P - HEADS)):
+            nc.sync.dma_start(
+                out=out_1[w].rearrange("h n e -> h (n e)"),
+                in_=qk_by_row[row : row + HEADS].rearrange("c n e -> c (n e)"),
+            )
+
+        v_rows = v_by_feature[:, :, ROW0 : ROW0 + ROWS].rearrange("p e (w h) -> p e w h", w=WINDOWS)
+        for part, (first, width) in enumerate(V_PARTS):
+            v_pieces = [[(first, v_sums[w][part][:, :width])] for w in range(WINDOWS)]
+            for axis in range(AXES):
+                add_bias_axis(nc, axis, v_rows, v_pieces, bias_all[:, 2])
+        flip(
+            nc, psum, v_by_feature, v_by_row, identity, 0, HEAD_DIM,
+            [nc.vector.tensor_copy, nc.scalar.copy] * 3,
+        )
+        nc.sync.dma_start(
+            out=out_2.rearrange("w h n e -> (w h) (n e)"),
+            in_=v_by_row[ROW0 : ROW0 + ROWS].rearrange("c n e -> c (n e)"),
         )

@@ -226,9 +226,9 @@ def tile_windowattention_pa_k_kernel(
             keep.tile([P, COLUMNS], U8, align_bytes=64, name="planes%d" % slot)
             for slot in range(SLOTS)
         ]
-        bias_rows = load_bias(nc, consts, qkv_b)
         for slot in range(SLOTS):
             nc.vector.memset(planes[slot][:].bitcast(I32), 0)
+        bias_rows = load_bias(nc, consts, qkv_b)
         w_by_partition = qkv_w_words.rearrange("g p n t -> p g (n t)")
 
         x_words = {}
@@ -303,7 +303,8 @@ def tile_windowattention_pa_k_kernel(
         v_by_row = keep.tile([P, P, HEAD_DIM], F32)
 
         load_x(0, W_PASSES)
-        load_scales(0)
+        for slot in range(SLOTS):
+            load_scales(slot)
         w_next = load_w(0, W_PASSES, 0, QK_COLUMNS)
         load_x(W_PASSES, W_PASSES)
         bias_all = spread_bias(nc, consts, psum, bias_rows)
@@ -316,7 +317,6 @@ def tile_windowattention_pa_k_kernel(
             if after < PASSES:
                 if after % LANES == 0:
                     load_x(after, LANES)
-                    load_scales(after // LANES)
                 w_next = load_w(after, W_PASSES, 0, QK_COLUMNS)
                 for g in range(after, after + W_PASSES):
                     quantise_pass(g)

@@ -49,7 +49,7 @@ FLOPS = 2 * WINDOWS * P * K * COLUMNS
 
 def load_bias(nc, consts, qkv_b):
     bias_rows = consts.tile([P, COLUMNS], BF16)
-    nc.vector.memset(bias_rows[:].bitcast(I32), 0)
+    nc.gpsimd.memset(bias_rows[:].bitcast(I32), 0)
     nc.scalar.dma_start(out=bias_rows[0:1, :], in_=qkv_b.rearrange("(o n) -> o n", o=1))
     return bias_rows
 
@@ -210,7 +210,7 @@ def tile_windowattention_pa_k_kernel(
         stack.enter_context(tc.manual_schedule())
         consts = stack.enter_context(tc.tile_pool(name="consts", bufs=1))
         keep = stack.enter_context(tc.tile_pool(name="keep", bufs=1))
-        x_pool = stack.enter_context(tc.tile_pool(name="x_pool", bufs=3))
+        x_pool = stack.enter_context(tc.tile_pool(name="x_pool", bufs=2))
         stage = stack.enter_context(tc.tile_pool(name="stage", bufs=4))
         weights = stack.enter_context(tc.tile_pool(name="weights", bufs=7))
         work = stack.enter_context(tc.tile_pool(name="work", bufs=1))
@@ -219,6 +219,7 @@ def tile_windowattention_pa_k_kernel(
         def bank(i):
             return psum.tile([P, BANK], F32, tag="bank%d" % i, name="bank")
 
+        bias_rows = load_bias(nc, consts, qkv_b)
         identity = consts.tile([P, P], F32)
         make_identity(nc, identity[:])
 
@@ -228,9 +229,9 @@ def tile_windowattention_pa_k_kernel(
         ]
         for slot in range(SLOTS):
             nc.vector.memset(planes[slot][:].bitcast(I32), 0)
-        bias_rows = load_bias(nc, consts, qkv_b)
         w_by_partition = qkv_w_words.rearrange("g p n t -> p g (n t)")
 
+        x_sorted = {}
         x_words = {}
 
         def load_x(pass0, passes):
@@ -264,14 +265,22 @@ def tile_windowattention_pa_k_kernel(
         x_codes = keep.tile([P, PASSES, WINDOWS * P], U32, align_bytes=64)
         x_scales = keep.tile([P, PASSES, WINDOWS * P], U8, align_bytes=64)
 
+        def sort_words(pass0):
+            words_sorted = x_pool.tile([P, WINDOWS, W_PASSES, 2, P], F32, name="words_sorted")
+            for i in range(W_PASSES):
+                nc.vector.tensor_copy(
+                    out=words_sorted[:, :, i],
+                    in_=x_words[pass0 + i].bitcast(F32).rearrange("p w (r u) -> p w u r", u=2),
+                )
+                x_sorted[pass0 + i] = words_sorted[:, :, i]
+
         def quantise_pass(g):
             flipped = bank(X_BANKS[g % 2])[:].rearrange("p (w u r) -> p w u r", w=WINDOWS, u=2)
             for w in range(WINDOWS):
-                words = x_words[g][:, w, :].bitcast(F32)
                 for u in range(2):
                     nc.tensor.transpose(
                         out=flipped[:, w, u, :],
-                        in_=words[:, u::2],
+                        in_=x_sorted[g][:, w, u, :],
                         identity=identity[:],
                     )
             grouped = stage.tile([P, WINDOWS * P * 4], BF16, align_bytes=64, name="grouped")
@@ -303,10 +312,12 @@ def tile_windowattention_pa_k_kernel(
         v_by_row = keep.tile([P, P, HEAD_DIM], F32)
 
         load_x(0, W_PASSES)
+        load_x(W_PASSES, W_PASSES)
         for slot in range(SLOTS):
             load_scales(slot)
         w_next = load_w(0, W_PASSES, 0, QK_COLUMNS)
-        load_x(W_PASSES, W_PASSES)
+        sort_words(0)
+        sort_words(W_PASSES)
         bias_all = spread_bias(nc, consts, psum, bias_rows)
         for g in range(W_PASSES):
             quantise_pass(g)
@@ -315,9 +326,12 @@ def tile_windowattention_pa_k_kernel(
             words = w_next
             after = pass0 + W_PASSES
             if after < PASSES:
-                if after % LANES == 0:
-                    load_x(after, LANES)
+                ahead = after + W_PASSES
+                if ahead < PASSES and ahead % LANES == 0:
+                    load_x(ahead, LANES)
                 w_next = load_w(after, W_PASSES, 0, QK_COLUMNS)
+                if ahead < PASSES:
+                    sort_words(ahead)
                 for g in range(after, after + W_PASSES):
                     quantise_pass(g)
             if pass0 == 0:
@@ -325,7 +339,9 @@ def tile_windowattention_pa_k_kernel(
                     for part in range(QK_PARTS):
                         qk_sums[w][part] = bank(QK_BANKS[w][part])
                 cos_table, sin_table = rotation_tables(nc, consts)
-                nc.vector.memset(v_by_feature[:], 0.0)
+            if pass0 in (2 * W_PASSES, 3 * W_PASSES):
+                side = 0 if pass0 == 2 * W_PASSES else ROW0 + ROWS
+                nc.vector.memset(v_by_feature[:, :, side : side + ROW0], 0.0)
             steps = [
                 (i, w, part)
                 for i in range(W_PASSES)

@@ -36,6 +36,8 @@ PER_BANK = BANK // P
 QK_COLUMNS = 2 * SECTION
 QK_PARTS = QK_COLUMNS // BANK
 V_PARTS = ((0, 512), (512, 256))
+V_GROUPS = ((4,), (4,), (4,), (2,), (1, 1))
+V_FLIP_PASS = 12
 X_BANKS = (0, 1)
 QK_BANKS = ((2, 3, 4), (5, 6, 7))
 V_BANKS = ((0, 2), (1, 5))
@@ -379,32 +381,37 @@ def tile_windowattention_pa_k_kernel(
             rotate(nc, work, rows, y, cos_table[:, section], sin_table[:, section])
 
         v_sums = [[bank(V_BANKS[w][0]), None] for w in range(WINDOWS)]
-        for slot in range(SLOTS):
-            words = load_w(slot * LANES, LANES, QK_COLUMNS, SECTION)
+        pass0 = 0
+        for loads in V_GROUPS:
+            if pass0 == V_FLIP_PASS:
+                flip(
+                    nc, psum, qk_by_feature, qk_by_row, identity, 0, HEAD_DIM,
+                    [nc.scalar.copy] * 6,
+                )
+            group = []
+            for passes in loads:
+                words = load_w(pass0, passes, QK_COLUMNS, SECTION)
+                group += [(pass0 + i, words[:, i, :]) for i in range(passes)]
+                pass0 += passes
             for part, (first, width) in enumerate(V_PARTS):
-                if slot == 0 and part == 1:
+                if group[0][0] == 0 and part == 1:
                     for w in range(WINDOWS):
                         v_sums[w][1] = bank(V_BANKS[w][1])
-                if slot == SLOTS - 1 and part == 1:
-                    flip(
-                        nc, psum, qk_by_feature, qk_by_row, identity, 0, HEAD_DIM,
-                        [nc.scalar.copy] * 6,
-                    )
-                for lane in range(LANES):
+                for g, words in group:
                     for w in range(WINDOWS):
                         multiply(
-                            slot * LANES + lane,
+                            g,
                             w,
                             v_sums[w][part][:, :width],
-                            words[:, lane, first : first + width],
+                            words[:, first : first + width],
                             QK_COLUMNS + first,
                         )
         nc.sync.dma_start(
             out=out_0.rearrange("w h n e -> (w h) (n e)"),
             in_=qk_by_row[ROW0 : ROW0 + ROWS].rearrange("c n e -> c (n e)"),
         )
-        for w, row in ((0, 0), (1, P - HEADS)):
-            nc.sync.dma_start(
+        for queue, w, row in ((nc.sync, 0, 0), (nc.scalar, 1, P - HEADS)):
+            queue.dma_start(
                 out=out_1[w].rearrange("h n e -> h (n e)"),
                 in_=qk_by_row[row : row + HEADS].rearrange("c n e -> c (n e)"),
             )

@@ -238,10 +238,10 @@ def tile_windowattention_pa_k_kernel(
 
         def load_x(pass0, passes):
             raw = x_pool.tile([P, WINDOWS, passes * K_PASS], BF16, tag="x", name="x_raw")
-            for w in range(WINDOWS):
-                nc.sync.dma_start(
-                    out=raw[:, w, :], in_=x[w, :, pass0 * K_PASS : (pass0 + passes) * K_PASS]
-                )
+            nc.sync.dma_start(
+                out=raw[:],
+                in_=x[:, :, pass0 * K_PASS : (pass0 + passes) * K_PASS].rearrange("w n k -> n w k"),
+            )
             for i in range(passes):
                 x_words[pass0 + i] = raw[:, :, i * K_PASS : (i + 1) * K_PASS]
 
@@ -317,7 +317,7 @@ def tile_windowattention_pa_k_kernel(
         load_x(W_PASSES, W_PASSES)
         for slot in range(SLOTS):
             load_scales(slot)
-        w_next = load_w(0, W_PASSES, 0, QK_COLUMNS)
+        w_next = [load_w(g, 1, 0, QK_COLUMNS)[:, 0, :] for g in range(W_PASSES)]
         sort_words(0)
         sort_words(W_PASSES)
         bias_all = spread_bias(nc, consts, psum, bias_rows)
@@ -331,7 +331,8 @@ def tile_windowattention_pa_k_kernel(
                 ahead = after + W_PASSES
                 if ahead < PASSES and ahead % LANES == 0:
                     load_x(ahead, LANES)
-                w_next = load_w(after, W_PASSES, 0, QK_COLUMNS)
+                w_pair = load_w(after, W_PASSES, 0, QK_COLUMNS)
+                w_next = [w_pair[:, i, :] for i in range(W_PASSES)]
                 if ahead < PASSES:
                     sort_words(ahead)
                 for g in range(after, after + W_PASSES):
@@ -357,7 +358,7 @@ def tile_windowattention_pa_k_kernel(
                     pass0 + i,
                     w,
                     qk_sums[w][part][:],
-                    words[:, i, part * BANK : (part + 1) * BANK],
+                    words[i][:, part * BANK : (part + 1) * BANK],
                     part * BANK,
                 )
 
@@ -390,20 +391,29 @@ def tile_windowattention_pa_k_kernel(
                 )
             group = []
             for passes in loads:
-                words = load_w(pass0, passes, QK_COLUMNS, SECTION)
-                group += [(pass0 + i, words[:, i, :]) for i in range(passes)]
+                if pass0 == PASSES - 1:
+                    parts = [
+                        load_w(pass0, 1, QK_COLUMNS + first, width)[:, 0, :]
+                        for first, width in V_PARTS
+                    ]
+                    group.append((pass0, parts))
+                else:
+                    words = load_w(pass0, passes, QK_COLUMNS, SECTION)
+                    for i in range(passes):
+                        parts = [words[:, i, first : first + width] for first, width in V_PARTS]
+                        group.append((pass0 + i, parts))
                 pass0 += passes
             for part, (first, width) in enumerate(V_PARTS):
                 if group[0][0] == 0 and part == 1:
                     for w in range(WINDOWS):
                         v_sums[w][1] = bank(V_BANKS[w][1])
-                for g, words in group:
+                for g, parts in group:
                     for w in range(WINDOWS):
                         multiply(
                             g,
                             w,
                             v_sums[w][part][:, :width],
-                            words[:, first : first + width],
+                            parts[part],
                             QK_COLUMNS + first,
                         )
         nc.sync.dma_start(

@@ -46,6 +46,8 @@ W_PASSES = 2
 ROW0 = 32
 BIAS_FEATURES = 12
 
+ALIGN = 256
+
 FLOPS = 2 * WINDOWS * P * K * COLUMNS
 
 
@@ -226,7 +228,7 @@ def tile_windowattention_pa_k_kernel(
         make_identity(nc, identity[:])
 
         planes = [
-            keep.tile([P, COLUMNS], U8, align_bytes=64, name="planes%d" % slot)
+            keep.tile([P, COLUMNS], U8, align_bytes=ALIGN, name="planes%d" % slot)
             for slot in range(SLOTS)
         ]
         for slot in range(SLOTS):
@@ -237,7 +239,9 @@ def tile_windowattention_pa_k_kernel(
         x_words = {}
 
         def load_x(pass0, passes):
-            raw = x_pool.tile([P, WINDOWS, passes * K_PASS], BF16, tag="x", name="x_raw")
+            raw = x_pool.tile(
+                [P, WINDOWS, passes * K_PASS], BF16, tag="x", name="x_raw", align_bytes=ALIGN
+            )
             nc.sync.dma_start(
                 out=raw[:],
                 in_=x[:, :, pass0 * K_PASS : (pass0 + passes) * K_PASS].rearrange("w n k -> n w k"),
@@ -255,7 +259,7 @@ def tile_windowattention_pa_k_kernel(
                 )
 
         def load_w(pass0, passes, column0, columns):
-            words = weights.tile([P, passes, columns], U32, align_bytes=64, tag="w", name="w_words")
+            words = weights.tile([P, passes, columns], U32, align_bytes=ALIGN, tag="w", name="w_words")
             nc.sync.dma_start(
                 out=words[:].bitcast(I32),
                 in_=w_by_partition[
@@ -264,8 +268,8 @@ def tile_windowattention_pa_k_kernel(
             )
             return words
 
-        x_codes = keep.tile([P, PASSES, WINDOWS * P], U32, align_bytes=64)
-        x_scales = keep.tile([P, PASSES, WINDOWS * P], U8, align_bytes=64)
+        x_codes = keep.tile([P, PASSES, WINDOWS * P], U32, align_bytes=ALIGN)
+        x_scales = keep.tile([P, PASSES, WINDOWS * P], U8, align_bytes=ALIGN)
 
         def sort_words(pass0):
             words_sorted = x_pool.tile([P, WINDOWS, W_PASSES, 2, P], F32, name="words_sorted")
@@ -285,7 +289,7 @@ def tile_windowattention_pa_k_kernel(
                         in_=x_sorted[g][:, w, u, :],
                         identity=identity[:],
                     )
-            grouped = stage.tile([P, WINDOWS * P * 4], BF16, align_bytes=64, name="grouped")
+            grouped = stage.tile([P, WINDOWS * P * 4], BF16, align_bytes=ALIGN, name="grouped")
             nc.scalar.copy(
                 out=grouped[:].bitcast(F32).rearrange("p (w r u) -> p w r u", w=WINDOWS, u=2),
                 in_=flipped.rearrange("p w u r -> p w r u"),
@@ -309,9 +313,9 @@ def tile_windowattention_pa_k_kernel(
             )
 
         qk_by_feature = keep.tile([P, HEAD_DIM, P], F32)
-        qk_by_row = keep.tile([P, P, HEAD_DIM], F32)
+        qk_by_row = keep.tile([P, P, HEAD_DIM], F32, align_bytes=ALIGN)
         v_by_feature = keep.tile([P, HEAD_DIM, P], F32)
-        v_by_row = keep.tile([P, P, HEAD_DIM], F32)
+        v_by_row = keep.tile([P, P, HEAD_DIM], F32, align_bytes=ALIGN)
 
         load_x(0, W_PASSES)
         load_x(W_PASSES, W_PASSES)
@@ -320,31 +324,25 @@ def tile_windowattention_pa_k_kernel(
         w_next = [load_w(g, 1, 0, QK_COLUMNS)[:, 0, :] for g in range(W_PASSES)]
         sort_words(0)
         sort_words(W_PASSES)
-        bias_all = spread_bias(nc, consts, psum, bias_rows)
         for g in range(W_PASSES):
+            quantise_pass(g)
+        bias_all = spread_bias(nc, consts, psum, bias_rows)
+        for g in range(W_PASSES, 2 * W_PASSES):
             quantise_pass(g)
         qk_sums = [[None] * QK_PARTS for w in range(WINDOWS)]
         for pass0 in range(0, PASSES, W_PASSES):
             words = w_next
             after = pass0 + W_PASSES
             if after < PASSES:
+                w_pair = load_w(after, W_PASSES, 0, QK_COLUMNS)
+                w_next = [w_pair[:, i, :] for i in range(W_PASSES)]
                 ahead = after + W_PASSES
                 if ahead < PASSES and ahead % LANES == 0:
                     load_x(ahead, LANES)
-                w_pair = load_w(after, W_PASSES, 0, QK_COLUMNS)
-                w_next = [w_pair[:, i, :] for i in range(W_PASSES)]
-                if ahead < PASSES:
-                    sort_words(ahead)
-                for g in range(after, after + W_PASSES):
-                    quantise_pass(g)
             if pass0 == 0:
                 for w in range(WINDOWS):
                     for part in range(QK_PARTS):
                         qk_sums[w][part] = bank(QK_BANKS[w][part])
-                cos_table, sin_table = rotation_tables(nc, consts)
-            if pass0 in (2 * W_PASSES, 3 * W_PASSES):
-                side = 0 if pass0 == 2 * W_PASSES else ROW0 + ROWS
-                nc.vector.memset(v_by_feature[:, :, side : side + ROW0], 0.0)
             steps = [
                 (i, w, part)
                 for i in range(W_PASSES)
@@ -353,7 +351,13 @@ def tile_windowattention_pa_k_kernel(
             ]
             if after == PASSES:
                 steps = sorted(steps, key=lambda step: step[2])
-            for i, w, part in steps:
+            for n, (i, w, part) in enumerate(steps):
+                if after < PASSES and n == len(steps) // 2:
+                    if pass0 > 0:
+                        for g in range(after, after + W_PASSES):
+                            quantise_pass(g)
+                    if ahead < PASSES:
+                        sort_words(ahead)
                 multiply(
                     pass0 + i,
                     w,
@@ -361,6 +365,11 @@ def tile_windowattention_pa_k_kernel(
                     words[i][:, part * BANK : (part + 1) * BANK],
                     part * BANK,
                 )
+            if pass0 == 0:
+                cos_table, sin_table = rotation_tables(nc, consts)
+            if pass0 in (2 * W_PASSES, 3 * W_PASSES):
+                side = 0 if pass0 == 2 * W_PASSES else ROW0 + ROWS
+                nc.vector.memset(v_by_feature[:, :, side : side + ROW0], 0.0)
 
         half_bank = BANK // 2
         q_pieces = [

@@ -36,8 +36,8 @@ PER_BANK = BANK // P
 QK_COLUMNS = 2 * SECTION
 QK_PARTS = QK_COLUMNS // BANK
 V_PARTS = ((0, 512), (512, 256))
-V_GROUPS = ((4,), (4,), (4,), (2,), (1, 1))
-V_FLIP_PASS = 12
+V_LOADS = ((0, 4, (0, 1)), (4, 4, (0, 1)), (8, 4, (0, 1)), (12, 4, (0,)), (12, 3, (1,)), (15, 1, (1,)))
+V_FLIP_LOAD = 3
 X_BANKS = (0, 1)
 QK_BANKS = ((2, 3, 4), (5, 6, 7))
 V_BANKS = ((0, 2), (1, 5))
@@ -60,7 +60,7 @@ def load_bias(nc, consts, qkv_b):
 
 def spread_bias(nc, consts, psum, bias_rows):
     ones = consts.tile([P, P], BF16)
-    nc.vector.memset(ones[:], 1.0)
+    nc.gpsimd.memset(ones[:], 1.0)
     bias_all = consts.tile([P, SECTIONS, HEAD_DIM, HEADS], F32)
     block = 0
     for section in range(SECTIONS):
@@ -317,8 +317,7 @@ def tile_windowattention_pa_k_kernel(
         v_by_feature = keep.tile([P, HEAD_DIM, P], F32)
         v_by_row = keep.tile([P, P, HEAD_DIM], F32, align_bytes=ALIGN)
 
-        load_x(0, W_PASSES)
-        load_x(W_PASSES, W_PASSES)
+        load_x(0, LANES)
         for slot in range(SLOTS):
             load_scales(slot)
         w_next = [load_w(g, 1, 0, QK_COLUMNS)[:, 0, :] for g in range(W_PASSES)]
@@ -391,38 +390,26 @@ def tile_windowattention_pa_k_kernel(
             rotate(nc, work, rows, y, cos_table[:, section], sin_table[:, section])
 
         v_sums = [[bank(V_BANKS[w][0]), None] for w in range(WINDOWS)]
-        pass0 = 0
-        for loads in V_GROUPS:
-            if pass0 == V_FLIP_PASS:
+        for n, (pass0, passes, parts) in enumerate(V_LOADS):
+            if n == V_FLIP_LOAD:
                 flip(
                     nc, psum, qk_by_feature, qk_by_row, identity, 0, HEAD_DIM,
                     [nc.scalar.copy] * 6,
                 )
-            group = []
-            for passes in loads:
-                if pass0 == PASSES - 1:
-                    parts = [
-                        load_w(pass0, 1, QK_COLUMNS + first, width)[:, 0, :]
-                        for first, width in V_PARTS
-                    ]
-                    group.append((pass0, parts))
-                else:
-                    words = load_w(pass0, passes, QK_COLUMNS, SECTION)
-                    for i in range(passes):
-                        parts = [words[:, i, first : first + width] for first, width in V_PARTS]
-                        group.append((pass0 + i, parts))
-                pass0 += passes
-            for part, (first, width) in enumerate(V_PARTS):
-                if group[0][0] == 0 and part == 1:
+            column0 = V_PARTS[parts[0]][0]
+            words = load_w(pass0, passes, QK_COLUMNS + column0, sum(V_PARTS[part][1] for part in parts))
+            for part in parts:
+                first, width = V_PARTS[part]
+                if pass0 == 0 and part == 1:
                     for w in range(WINDOWS):
                         v_sums[w][1] = bank(V_BANKS[w][1])
-                for g, parts in group:
+                for i in range(passes):
                     for w in range(WINDOWS):
                         multiply(
-                            g,
+                            pass0 + i,
                             w,
                             v_sums[w][part][:, :width],
-                            parts[part],
+                            words[:, i, first - column0 : first - column0 + width],
                             QK_COLUMNS + first,
                         )
         nc.sync.dma_start(

@@ -36,16 +36,19 @@ PER_BANK = BANK // P
 QK_COLUMNS = 2 * SECTION
 QK_PARTS = QK_COLUMNS // BANK
 V_PARTS = ((0, 512), (512, 256))
-V_LOADS = ((0, 4, (0, 1)), (4, 4, (0, 1)), (8, 4, (0, 1)), (12, 4, (0,)), (12, 3, (1,)), (15, 1, (1,)))
-V_FLIP_LOAD = 3
+V_LOADS = ((0, 4, (0, 1)), (4, 4, (0, 1)), (8, 4, (0, 1)), (12, 4, (0,)), (12, 4, (1,)))
 X_BANKS = (0, 1)
 QK_BANKS = ((2, 3, 4), (5, 6, 7))
 V_BANKS = ((0, 2), (1, 5))
-FLIP_BANKS = (3, 6, 4, 7)
 W_PASSES = 2
 ROW0 = 32
 BIAS_FEATURES = 12
 
+SQUARE = 32
+BLOCKS = P // SQUARE
+RUN = 4
+RUNS = HEAD_DIM // RUN
+VECTOR_AXES = 1
 ALIGN = 256
 
 FLOPS = 2 * WINDOWS * P * K * COLUMNS
@@ -150,59 +153,82 @@ def rotation_tables(nc, consts):
     return cos_table, sin_table
 
 
-def add_bias_axis(nc, axis, target, pieces, bias_section):
+def add_bias(nc, axis, w, target, pieces, bias_section):
     features = slice(GROUP * axis, GROUP * (axis + 1))
-    for w in range(WINDOWS):
-        for first, sums in pieces[w]:
-            width = sums.shape[1]
-            groups = sums.rearrange("p (g f) -> p g f", f=GROUP)
-            start = (axis - first // GROUP) % AXES
-            head0 = (first // GROUP + start) // AXES
-            heads = len(range(start, width // GROUP, AXES))
-            nc.vector.tensor_add(
-                out=target[:, features, w, head0 : head0 + heads],
-                in0=groups[:, start : width // GROUP : AXES, :].rearrange("p h f -> p f h"),
-                in1=bias_section[:, features, head0 : head0 + heads],
-            )
+    for first, sums in pieces:
+        width = sums.shape[1]
+        groups = sums.rearrange("p (g f) -> p g f", f=GROUP)
+        start = (axis - first // GROUP) % AXES
+        head0 = (first // GROUP + start) // AXES
+        heads = len(range(start, width // GROUP, AXES))
+        nc.vector.tensor_add(
+            out=target[:, w, features, head0 : head0 + heads],
+            in0=groups[:, start : width // GROUP : AXES, :].rearrange("p h f -> p f h"),
+            in1=bias_section[:, features, head0 : head0 + heads],
+        )
 
 
-def rotate(nc, work, target, y, cos_rows, sin_rows):
-    straight = work.tile([P, HEAD_DIM, ROWS], F32, name="straight")
-    crossed = work.tile([P, AXES, 2, PAIRS, ROWS], F32, name="crossed")
-    halves = y[:].rearrange("p (a s i) c -> p a s i c", a=AXES, s=2)
-    straight_halves = straight[:].rearrange("p (a s i) c -> p a s i c", a=AXES, s=2)
+def straight_products(nc, work, section, y, cos_rows):
+    straight = work.tile(
+        [P, WINDOWS, HEAD_DIM, HEADS], F32, tag="straight%d" % section, name="straight", align_bytes=ALIGN
+    )
     for axis in range(AXES):
         for pair in range(PAIRS):
+            feature = axis * GROUP + pair
+            both = slice(feature, feature + PAIRS + 1, PAIRS)
             nc.scalar.activation(
-                out=straight_halves[:, axis, :, pair, :],
-                in_=halves[:, axis, :, pair, :],
+                out=straight[:, :, both, :],
+                in_=y[:, :, both, :],
                 func=ACT.Copy,
                 scale=cos_rows[:, axis, 0, pair : pair + 1],
             )
-    for half in range(2):
-        nc.vector.tensor_mul(
-            out=crossed[:, :, half],
-            in0=halves[:, :, 1 - half],
-            in1=sin_rows[:, :, half, :].unsqueeze(3).to_broadcast([P, AXES, PAIRS, ROWS]),
-        )
-    nc.vector.tensor_add(
-        out=target,
-        in0=straight[:].rearrange("p e (w h) -> p e w h", w=WINDOWS),
-        in1=crossed[:].rearrange("p a s i (w h) -> p (a s i) w h", w=WINDOWS),
+    return straight
+
+
+def crossed_products(nc, work, section, y, sin_rows):
+    crossed = work.tile(
+        [P, WINDOWS, HEAD_DIM, HEADS], F32, tag="crossed%d" % section, name="crossed", align_bytes=ALIGN
+    )
+    for axis in range(AXES):
+        for half in range(2):
+            first = axis * GROUP + half * PAIRS
+            partner = axis * GROUP + (1 - half) * PAIRS
+            if axis < VECTOR_AXES:
+                nc.vector.tensor_mul(
+                    out=crossed[:, :, first : first + PAIRS, :],
+                    in0=y[:, :, partner : partner + PAIRS, :],
+                    in1=sin_rows[:, axis, half, :]
+                    .unsqueeze(1)
+                    .unsqueeze(3)
+                    .to_broadcast([P, WINDOWS, PAIRS, HEADS]),
+                )
+                continue
+            for pair in range(PAIRS):
+                nc.scalar.activation(
+                    out=crossed[:, :, first + pair, :],
+                    in_=y[:, :, partner + pair, :],
+                    func=ACT.Copy,
+                    scale=sin_rows[:, axis, half, pair : pair + 1],
+                )
+    return crossed
+
+
+def sort_rows(copy, by_row, turned, w, runs):
+    features = slice(runs[0] * RUN, runs[1] * RUN)
+    copy(
+        out=by_row[:, w, :, features].rearrange("p t (r e) -> p r t e", e=RUN),
+        in_=turned[:, w, features, :].rearrange("p (r e) t -> p r t e", e=RUN),
     )
 
 
-def flip(nc, psum, by_feature, by_row, identity, first_feature, features, copies):
-    for i, first in enumerate(range(first_feature, first_feature + features, PER_BANK)):
-        bank = FLIP_BANKS[(first // PER_BANK) % len(FLIP_BANKS)]
-        flipped = psum.tile([P, PER_BANK, P], F32, tag="bank%d" % bank, name="flipped")
-        for e in range(PER_BANK):
-            nc.tensor.transpose(
-                out=flipped[:, e, :], in_=by_feature[:, first + e, :], identity=identity[:]
-            )
-        copies[i](
-            out=by_row[:, :, first : first + PER_BANK],
-            in_=flipped[:].rearrange("c e n -> c n e"),
+def store(nc, by_row, out):
+    for block in range(BLOCKS):
+        queue = nc.sync if block < BLOCKS // 2 else nc.scalar
+        queue.dma_start(
+            out=out[:, :, block * SQUARE : (block + 1) * SQUARE, :].rearrange(
+                "w h n e -> h w (n e)"
+            ),
+            in_=by_row[block * SQUARE : (block + 1) * SQUARE].rearrange("h w n e -> h w (n e)"),
         )
 
 
@@ -312,11 +338,6 @@ def tile_windowattention_pa_k_kernel(
                 stop=(g == PASSES - 1),
             )
 
-        qk_by_feature = keep.tile([P, HEAD_DIM, P], F32)
-        qk_by_row = keep.tile([P, P, HEAD_DIM], F32, align_bytes=ALIGN)
-        v_by_feature = keep.tile([P, HEAD_DIM, P], F32)
-        v_by_row = keep.tile([P, P, HEAD_DIM], F32, align_bytes=ALIGN)
-
         load_x(0, LANES)
         for slot in range(SLOTS):
             load_scales(slot)
@@ -366,9 +387,6 @@ def tile_windowattention_pa_k_kernel(
                 )
             if pass0 == 0:
                 cos_table, sin_table = rotation_tables(nc, consts)
-            if pass0 in (2 * W_PASSES, 3 * W_PASSES):
-                side = 0 if pass0 == 2 * W_PASSES else ROW0 + ROWS
-                nc.vector.memset(v_by_feature[:, :, side : side + ROW0], 0.0)
 
         half_bank = BANK // 2
         q_pieces = [
@@ -378,24 +396,53 @@ def tile_windowattention_pa_k_kernel(
             [(0, qk_sums[w][1][:, half_bank:]), (half_bank, qk_sums[w][2][:])]
             for w in range(WINDOWS)
         ]
-        q_rows = qk_by_feature[:, :, ROW0 : ROW0 + ROWS].rearrange(
-            "p e (w h) -> p e w h", w=WINDOWS
-        )
-        k_rows = qk_by_feature[:].rearrange("p e (w h) -> p e w h", h=HEADS)[:, :, 0:4:3, :]
-        for section, pieces, rows in ((0, q_pieces, q_rows), (1, k_pieces, k_rows)):
-            y = work.tile([P, HEAD_DIM, ROWS], F32, name="y")
-            y_by_window = y[:].rearrange("p e (w h) -> p e w h", w=WINDOWS)
+
+        def biased(section, pieces):
+            y = work.tile(
+                [P, WINDOWS, HEAD_DIM, HEADS], F32, tag="y%d" % section, name="y", align_bytes=ALIGN
+            )
             for axis in range(AXES):
-                add_bias_axis(nc, axis, y_by_window, pieces, bias_all[:, section])
-            rotate(nc, work, rows, y, cos_table[:, section], sin_table[:, section])
+                for w in range(WINDOWS):
+                    add_bias(nc, axis, w, y, pieces[w], bias_all[:, section])
+            return y
+
+        def turned_tile(section):
+            return work.tile(
+                [P, WINDOWS, HEAD_DIM, SQUARE], F32, tag="crossed%d" % section, name="turned", align_bytes=ALIGN
+            )
+
+        def by_row_tile(section):
+            return work.tile(
+                [P, WINDOWS, SQUARE, HEAD_DIM], F32, tag="y%d" % section, name="by_row", align_bytes=ALIGN
+            )
+
+        def rotate_and_turn(section, straight, crossed):
+            flat = "p w e h -> p (w e h)"
+            nc.vector.tensor_add(
+                out=straight[:].rearrange(flat),
+                in0=straight[:].rearrange(flat),
+                in1=crossed[:].rearrange(flat),
+            )
+            turned = turned_tile(section)
+            nc.vector.transpose(out=turned[:].rearrange(flat), in_=straight[:].rearrange(flat))
+            return turned
+
+        y_q = biased(0, q_pieces)
+        straight_q = straight_products(nc, work, 0, y_q, cos_table[:, 0])
+        crossed_q = crossed_products(nc, work, 0, y_q, sin_table[:, 0])
+        y_k = biased(1, k_pieces)
+        straight_k = straight_products(nc, work, 1, y_k, cos_table[:, 1])
+        turned_q = rotate_and_turn(0, straight_q, crossed_q)
+        crossed_k = crossed_products(nc, work, 1, y_k, sin_table[:, 1])
+        turned_k = rotate_and_turn(1, straight_k, crossed_k)
+        by_row_q = by_row_tile(0)
+        by_row_k = by_row_tile(1)
+        for by_row, turned in ((by_row_q, turned_q), (by_row_k, turned_k)):
+            for w in range(WINDOWS):
+                sort_rows(nc.scalar.copy, by_row, turned, w, (0, RUNS))
 
         v_sums = [[bank(V_BANKS[w][0]), None] for w in range(WINDOWS)]
-        for n, (pass0, passes, parts) in enumerate(V_LOADS):
-            if n == V_FLIP_LOAD:
-                flip(
-                    nc, psum, qk_by_feature, qk_by_row, identity, 0, HEAD_DIM,
-                    [nc.scalar.copy] * 6,
-                )
+        for pass0, passes, parts in V_LOADS:
             column0 = V_PARTS[parts[0]][0]
             words = load_w(pass0, passes, QK_COLUMNS + column0, sum(V_PARTS[part][1] for part in parts))
             for part in parts:
@@ -403,8 +450,8 @@ def tile_windowattention_pa_k_kernel(
                 if pass0 == 0 and part == 1:
                     for w in range(WINDOWS):
                         v_sums[w][1] = bank(V_BANKS[w][1])
-                for i in range(passes):
-                    for w in range(WINDOWS):
+                for w in range(WINDOWS):
+                    for i in range(passes):
                         multiply(
                             pass0 + i,
                             w,
@@ -412,26 +459,30 @@ def tile_windowattention_pa_k_kernel(
                             words[:, i, first - column0 : first - column0 + width],
                             QK_COLUMNS + first,
                         )
-        nc.sync.dma_start(
-            out=out_0.rearrange("w h n e -> (w h) (n e)"),
-            in_=qk_by_row[ROW0 : ROW0 + ROWS].rearrange("c n e -> c (n e)"),
-        )
-        for queue, w, row in ((nc.sync, 0, 0), (nc.scalar, 1, P - HEADS)):
-            queue.dma_start(
-                out=out_1[w].rearrange("h n e -> h (n e)"),
-                in_=qk_by_row[row : row + HEADS].rearrange("c n e -> c (n e)"),
-            )
+        store(nc, by_row_q, out_0)
+        store(nc, by_row_k, out_1)
 
-        v_rows = v_by_feature[:, :, ROW0 : ROW0 + ROWS].rearrange("p e (w h) -> p e w h", w=WINDOWS)
-        for part, (first, width) in enumerate(V_PARTS):
-            v_pieces = [[(first, v_sums[w][part][:, :width])] for w in range(WINDOWS)]
+        v_pieces = [
+            [[(first, v_sums[w][part][:, :width])] for part, (first, width) in enumerate(V_PARTS)]
+            for w in range(WINDOWS)
+        ]
+        y_v = work.tile(
+            [P, WINDOWS, HEAD_DIM, HEADS], F32, tag="straight0", name="y_v", align_bytes=ALIGN
+        )
+        turned_v = turned_tile(2)
+        by_row_v = by_row_tile(2)
+        for w in range(WINDOWS):
             for axis in range(AXES):
-                add_bias_axis(nc, axis, v_rows, v_pieces, bias_all[:, 2])
-        flip(
-            nc, psum, v_by_feature, v_by_row, identity, 0, HEAD_DIM,
-            [nc.vector.tensor_copy, nc.scalar.copy] * 3,
-        )
-        nc.sync.dma_start(
-            out=out_2.rearrange("w h n e -> (w h) (n e)"),
-            in_=v_by_row[ROW0 : ROW0 + ROWS].rearrange("c n e -> c (n e)"),
-        )
+                add_bias(nc, axis, w, y_v, v_pieces[w][0], bias_all[:, 2])
+        for w in range(WINDOWS):
+            for axis in range(AXES):
+                add_bias(nc, axis, w, y_v, v_pieces[w][1], bias_all[:, 2])
+            nc.vector.transpose(
+                out=turned_v[:, w].rearrange("p e t -> p (e t)"),
+                in_=y_v[:, w].rearrange("p e h -> p (e h)"),
+            )
+            if w == 0:
+                sort_rows(nc.scalar.copy, by_row_v, turned_v, w, (0, RUNS))
+        sort_rows(nc.scalar.copy, by_row_v, turned_v, 1, (0, RUNS // 3))
+        sort_rows(nc.vector.tensor_copy, by_row_v, turned_v, 1, (RUNS // 3, RUNS))
+        store(nc, by_row_v, out_2)

import math
from contextlib import ExitStack

import concourse.mybir as mybir
from concourse.masks import make_identity

F32 = mybir.dt.float32
BF16 = mybir.dt.bfloat16
I32 = mybir.dt.int32
U32 = mybir.dt.uint32
U8 = mybir.dt.uint8
FP8X4 = mybir.dt.float8_e4m3fn_x4
ALU = mybir.AluOpType
ACT = mybir.ActivationFunctionType

P = 128
WINDOWS = 2
K = 8192
K_PASS = 512
PASSES = K // K_PASS
HEADS = 32
HEAD_DIM = 24
AXES = 3
GROUP = HEAD_DIM // AXES
PAIRS = GROUP // 2
SECTION = HEADS * HEAD_DIM
SECTIONS = 3
COLUMNS = SECTIONS * SECTION
BANK = 512
BANKS = 8
LANES = 4
SLOTS = PASSES // LANES
ROWS = WINDOWS * HEADS
PER_BANK = BANK // P

QK_COLUMNS = 2 * SECTION
QK_PARTS = QK_COLUMNS // BANK
V_PARTS = ((0, 512), (512, 256))
V_LOADS = ((0, 4, (0, 1)), (4, 4, (0, 1)), (8, 4, (0, 1)), (12, 4, (0,)), (12, 4, (1,)))
X_BANKS = (0, 1)
QK_BANKS = ((2, 3, 4), (5, 6, 7))
V_BANKS = ((0, 2), (1, 5))
W_PASSES = 2
ROW0 = 32
BIAS_FEATURES = 12

SQUARE = 32
BLOCKS = P // SQUARE
RUN = 4
RUNS = HEAD_DIM // RUN
VECTOR_AXES = 1
ALIGN = 256

FLOPS = 2 * WINDOWS * P * K * COLUMNS


def load_bias(nc, consts, qkv_b):
    bias_rows = consts.tile([P, COLUMNS], BF16)
    nc.gpsimd.memset(bias_rows[:].bitcast(I32), 0)
    nc.scalar.dma_start(out=bias_rows[0:1, :], in_=qkv_b.rearrange("(o n) -> o n", o=1))
    return bias_rows


def spread_bias(nc, consts, psum, bias_rows):
    ones = consts.tile([P, P], BF16)
    nc.gpsimd.memset(ones[:], 1.0)
    bias_all = consts.tile([P, SECTIONS, HEAD_DIM, HEADS], F32)
    block = 0
    for section in range(SECTIONS):
        by_feature = bias_rows[:, section * SECTION : (section + 1) * SECTION].rearrange(
            "p (h e) -> p e h", e=HEAD_DIM
        )
        for first in range(0, HEAD_DIM, BIAS_FEATURES):
            summed = psum.tile([P, BANK], F32, tag="bank%d" % (2 + block), name="summed")
            width = BIAS_FEATURES * HEADS
            nc.tensor.matmul(
                out=summed[:, :width],
                lhsT=ones[:],
                rhs=by_feature[:, first : first + BIAS_FEATURES, :],
                start=True,
                stop=True,
            )
            nc.vector.tensor_copy(
                out=bias_all[:, section, first : first + BIAS_FEATURES, :].rearrange(
                    "p e h -> p (e h)"
                ),
                in_=summed[:, :width],
            )
            block += 1
    return bias_all


def rotation_tables(nc, consts):
    token = consts.tile([P, 1], I32)
    nc.gpsimd.iota(out=token[:], pattern=[[0, 1]], base=0, channel_multiplier=1)
    place_int = consts.tile([P, AXES], I32)
    nc.vector.tensor_single_scalar(
        out=place_int[:, 0:1], in_=token[:], scalar=6, op=ALU.logical_shift_right
    )
    nc.vector.tensor_scalar(
        out=place_int[:, 1:2],
        in0=token[:],
        scalar1=3,
        scalar2=7,
        op0=ALU.logical_shift_right,
        op1=ALU.bitwise_and,
    )
    nc.vector.tensor_single_scalar(
        out=place_int[:, 2:3], in_=token[:], scalar=7, op=ALU.bitwise_and
    )
    place = consts.tile([P, AXES], F32)
    nc.vector.tensor_copy(out=place[:], in_=place_int[:])

    angles = consts.tile([P, 2, AXES, PAIRS], F32)
    for pair in range(PAIRS):
        nc.vector.tensor_single_scalar(
            out=angles[:, 1, :, pair],
            in_=place[:],
            scalar=1.0 / (10000.0 ** (2 * pair / 8)),
            op=ALU.mult,
        )
    nc.vector.tensor_single_scalar(
        out=angles[:, 0], in_=angles[:, 1], scalar=math.pi / 2, op=ALU.add
    )
    turn = consts.tile([P, 2, AXES, PAIRS], F32)
    nc.vector.tensor_scalar(
        out=turn[:],
        in0=angles[:],
        scalar1=math.pi,
        scalar2=2 * math.pi,
        op0=ALU.is_gt,
        op1=ALU.mult,
    )
    nc.vector.tensor_sub(out=angles[:], in0=angles[:], in1=turn[:])
    cos_sin = consts.tile([P, 2, AXES, PAIRS], F32)
    nc.scalar.activation(out=cos_sin[:], in_=angles[:], func=ACT.Sin)

    cos_table = consts.tile([P, 2, AXES, 2, PAIRS], F32)
    sin_table = consts.tile([P, 2, AXES, 2, PAIRS], F32)
    for section, factor in enumerate((HEAD_DIM**-0.5, 1.0)):
        nc.vector.tensor_single_scalar(
            out=cos_table[:, section],
            in_=cos_sin[:, 0].unsqueeze(2).to_broadcast([P, AXES, 2, PAIRS]),
            scalar=factor,
            op=ALU.mult,
        )
        nc.vector.tensor_single_scalar(
            out=sin_table[:, section, :, 0, :], in_=cos_sin[:, 1], scalar=-factor, op=ALU.mult
        )
        nc.vector.tensor_single_scalar(
            out=sin_table[:, section, :, 1, :], in_=cos_sin[:, 1], scalar=factor, op=ALU.mult
        )
    return cos_table, sin_table


def add_bias(nc, axis, w, target, pieces, bias_section):
    features = slice(GROUP * axis, GROUP * (axis + 1))
    for first, sums in pieces:
        width = sums.shape[1]
        groups = sums.rearrange("p (g f) -> p g f", f=GROUP)
        start = (axis - first // GROUP) % AXES
        head0 = (first // GROUP + start) // AXES
        heads = len(range(start, width // GROUP, AXES))
        nc.vector.tensor_add(
            out=target[:, w, features, head0 : head0 + heads],
            in0=groups[:, start : width // GROUP : AXES, :].rearrange("p h f -> p f h"),
            in1=bias_section[:, features, head0 : head0 + heads],
        )


def straight_products(nc, work, section, y, cos_rows):
    straight = work.tile(
        [P, WINDOWS, HEAD_DIM, HEADS], F32, tag="straight%d" % section, name="straight", align_bytes=ALIGN
    )
    for axis in range(AXES):
        for pair in range(PAIRS):
            feature = axis * GROUP + pair
            both = slice(feature, feature + PAIRS + 1, PAIRS)
            nc.scalar.activation(
                out=straight[:, :, both, :],
                in_=y[:, :, both, :],
                func=ACT.Copy,
                scale=cos_rows[:, axis, 0, pair : pair + 1],
            )
    return straight


def crossed_products(nc, work, section, y, sin_rows):
    crossed = work.tile(
        [P, WINDOWS, HEAD_DIM, HEADS], F32, tag="crossed%d" % section, name="crossed", align_bytes=ALIGN
    )
    for axis in range(AXES):
        for half in range(2):
            first = axis * GROUP + half * PAIRS
            partner = axis * GROUP + (1 - half) * PAIRS
            if axis < VECTOR_AXES:
                nc.vector.tensor_mul(
                    out=crossed[:, :, first : first + PAIRS, :],
                    in0=y[:, :, partner : partner + PAIRS, :],
                    in1=sin_rows[:, axis, half, :]
                    .unsqueeze(1)
                    .unsqueeze(3)
                    .to_broadcast([P, WINDOWS, PAIRS, HEADS]),
                )
                continue
            for pair in range(PAIRS):
                nc.scalar.activation(
                    out=crossed[:, :, first + pair, :],
                    in_=y[:, :, partner + pair, :],
                    func=ACT.Copy,
                    scale=sin_rows[:, axis, half, pair : pair + 1],
                )
    return crossed


def sort_rows(copy, by_row, turned, w, runs):
    features = slice(runs[0] * RUN, runs[1] * RUN)
    copy(
        out=by_row[:, w, :, features].rearrange("p t (r e) -> p r t e", e=RUN),
        in_=turned[:, w, features, :].rearrange("p (r e) t -> p r t e", e=RUN),
    )


def store(nc, by_row, out):
    for block in range(BLOCKS):
        queue = nc.sync if block < BLOCKS // 2 else nc.scalar
        queue.dma_start(
            out=out[:, :, block * SQUARE : (block + 1) * SQUARE, :].rearrange(
                "w h n e -> h w (n e)"
            ),
            in_=by_row[block * SQUARE : (block + 1) * SQUARE].rearrange("h w n e -> h w (n e)"),
        )


def tile_windowattention_pa_k_kernel(
    tc, x, qkv_w_words, qkv_w_scales, qkv_b, out_0, out_1, out_2
):
    nc = tc.nc
    with ExitStack() as stack:
        stack.enter_context(tc.manual_schedule())
        consts = stack.enter_context(tc.tile_pool(name="consts", bufs=1))
        keep = stack.enter_context(tc.tile_pool(name="keep", bufs=1))
        x_pool = stack.enter_context(tc.tile_pool(name="x_pool", bufs=2))
        stage = stack.enter_context(tc.tile_pool(name="stage", bufs=4))
        weights = stack.enter_context(tc.tile_pool(name="weights", bufs=7))
        work = stack.enter_context(tc.tile_pool(name="work", bufs=1))
        psum = stack.enter_context(tc.psum_pool(name="psum", bufs=1))

        def bank(i):
            return psum.tile([P, BANK], F32, tag="bank%d" % i, name="bank")

        bias_rows = load_bias(nc, consts, qkv_b)
        identity = consts.tile([P, P], F32)
        make_identity(nc, identity[:])

        planes = [
            keep.tile([P, COLUMNS], U8, align_bytes=ALIGN, name="planes%d" % slot)
            for slot in range(SLOTS)
        ]
        for slot in range(SLOTS):
            nc.vector.memset(planes[slot][:].bitcast(I32), 0)
        w_by_partition = qkv_w_words.rearrange("g p n t -> p g (n t)")

        x_sorted = {}
        x_words = {}

        def load_x(pass0, passes):
            raw = x_pool.tile(
                [P, WINDOWS, passes * K_PASS], BF16, tag="x", name="x_raw", align_bytes=ALIGN
            )
            nc.sync.dma_start(
                out=raw[:],
                in_=x[:, :, pass0 * K_PASS : (pass0 + passes) * K_PASS].rearrange("w n k -> n w k"),
            )
            for i in range(passes):
                x_words[pass0 + i] = raw[:, :, i * K_PASS : (i + 1) * K_PASS]

        def load_scales(slot):
            for quadrant in range(4):
                nc.sync.dma_start(
                    out=planes[slot][32 * quadrant : 32 * quadrant + 4 * LANES, :].bitcast(I32),
                    in_=qkv_w_scales[
                        LANES * slot : LANES * (slot + 1), 4 * quadrant : 4 * quadrant + 4, :
                    ].bitcast(I32),
                )

        def load_w(pass0, passes, column0, columns):
            words = weights.tile([P, passes, columns], U32, align_bytes=ALIGN, tag="w", name="w_words")
            nc.sync.dma_start(
                out=words[:].bitcast(I32),
                in_=w_by_partition[
                    :, pass0 : pass0 + passes, 4 * column0 : 4 * (column0 + columns)
                ].bitcast(I32),
            )
            return words

        x_codes = keep.tile([P, PASSES, WINDOWS * P], U32, align_bytes=ALIGN)
        x_scales = keep.tile([P, PASSES, WINDOWS * P], U8, align_bytes=ALIGN)

        def sort_words(pass0):
            words_sorted = x_pool.tile([P, WINDOWS, W_PASSES, 2, P], F32, name="words_sorted")
            for i in range(W_PASSES):
                nc.vector.tensor_copy(
                    out=words_sorted[:, :, i],
                    in_=x_words[pass0 + i].bitcast(F32).rearrange("p w (r u) -> p w u r", u=2),
                )
                x_sorted[pass0 + i] = words_sorted[:, :, i]

        def quantise_pass(g):
            flipped = bank(X_BANKS[g % 2])[:].rearrange("p (w u r) -> p w u r", w=WINDOWS, u=2)
            for w in range(WINDOWS):
                for u in range(2):
                    nc.tensor.transpose(
                        out=flipped[:, w, u, :],
                        in_=x_sorted[g][:, w, u, :],
                        identity=identity[:],
                    )
            grouped = stage.tile([P, WINDOWS * P * 4], BF16, align_bytes=ALIGN, name="grouped")
            nc.scalar.copy(
                out=grouped[:].bitcast(F32).rearrange("p (w r u) -> p w r u", w=WINDOWS, u=2),
                in_=flipped.rearrange("p w u r -> p w r u"),
            )
            nc.vector.quantize_mx(
                out=x_codes[:, g, :].bitcast(FP8X4), scales=x_scales[:, g, :], in_=grouped[:]
            )

        def multiply(g, w, target, words, column):
            width = target.shape[1]
            tokens = slice(w * P, (w + 1) * P)
            slot, lane = divmod(g, LANES)
            nc.tensor.matmul_mx(
                out=target,
                lhsT=x_codes[:, g, tokens].bitcast(FP8X4),
                lhsT_scale=x_scales[:, g, tokens],
                rhs=words.bitcast(FP8X4),
                rhs_scale=planes[slot][4 * lane : P, column : column + width],
                start=(g == 0),
                stop=(g == PASSES - 1),
            )

        load_x(0, LANES)
        for slot in range(SLOTS):
            load_scales(slot)
        w_next = [load_w(g, 1, 0, QK_COLUMNS)[:, 0, :] for g in range(W_PASSES)]
        sort_words(0)
        sort_words(W_PASSES)
        for g in range(W_PASSES):
            quantise_pass(g)
        bias_all = spread_bias(nc, consts, psum, bias_rows)
        for g in range(W_PASSES, 2 * W_PASSES):
            quantise_pass(g)
        qk_sums = [[None] * QK_PARTS for w in range(WINDOWS)]
        for pass0 in range(0, PASSES, W_PASSES):
            words = w_next
            after = pass0 + W_PASSES
            if after < PASSES:
                w_pair = load_w(after, W_PASSES, 0, QK_COLUMNS)
                w_next = [w_pair[:, i, :] for i in range(W_PASSES)]
                ahead = after + W_PASSES
                if ahead < PASSES and ahead % LANES == 0:
                    load_x(ahead, LANES)
            if pass0 == 0:
                for w in range(WINDOWS):
                    for part in range(QK_PARTS):
                        qk_sums[w][part] = bank(QK_BANKS[w][part])
            steps = [
                (i, w, part)
                for i in range(W_PASSES)
                for w in range(WINDOWS)
                for part in range(QK_PARTS)
            ]
            if after == PASSES:
                steps = sorted(steps, key=lambda step: step[2])
            for n, (i, w, part) in enumerate(steps):
                if after < PASSES and n == len(steps) // 2:
                    if pass0 > 0:
                        for g in range(after, after + W_PASSES):
                            quantise_pass(g)
                    if ahead < PASSES:
                        sort_words(ahead)
                multiply(
                    pass0 + i,
                    w,
                    qk_sums[w][part][:],
                    words[i][:, part * BANK : (part + 1) * BANK],
                    part * BANK,
                )
            if pass0 == 0:
                cos_table, sin_table = rotation_tables(nc, consts)

        half_bank = BANK // 2
        q_pieces = [
            [(0, qk_sums[w][0][:]), (BANK, qk_sums[w][1][:, :half_bank])] for w in range(WINDOWS)
        ]
        k_pieces = [
            [(0, qk_sums[w][1][:, half_bank:]), (half_bank, qk_sums[w][2][:])]
            for w in range(WINDOWS)
        ]

        def biased(section, pieces):
            y = work.tile(
                [P, WINDOWS, HEAD_DIM, HEADS], F32, tag="y%d" % section, name="y", align_bytes=ALIGN
            )
            for axis in range(AXES):
                for w in range(WINDOWS):
                    add_bias(nc, axis, w, y, pieces[w], bias_all[:, section])
            return y

        def turned_tile(section):
            return work.tile(
                [P, WINDOWS, HEAD_DIM, SQUARE], F32, tag="crossed%d" % section, name="turned", align_bytes=ALIGN
            )

        def by_row_tile(section):
            return work.tile(
                [P, WINDOWS, SQUARE, HEAD_DIM], F32, tag="y%d" % section, name="by_row", align_bytes=ALIGN
            )

        def rotate_and_turn(section, straight, crossed):
            flat = "p w e h -> p (w e h)"
            nc.vector.tensor_add(
                out=straight[:].rearrange(flat),
                in0=straight[:].rearrange(flat),
                in1=crossed[:].rearrange(flat),
            )
            turned = turned_tile(section)
            nc.vector.transpose(out=turned[:].rearrange(flat), in_=straight[:].rearrange(flat))
            return turned

        y_q = biased(0, q_pieces)
        straight_q = straight_products(nc, work, 0, y_q, cos_table[:, 0])
        crossed_q = crossed_products(nc, work, 0, y_q, sin_table[:, 0])
        y_k = biased(1, k_pieces)
        straight_k = straight_products(nc, work, 1, y_k, cos_table[:, 1])
        turned_q = rotate_and_turn(0, straight_q, crossed_q)
        crossed_k = crossed_products(nc, work, 1, y_k, sin_table[:, 1])
        turned_k = rotate_and_turn(1, straight_k, crossed_k)
        by_row_q = by_row_tile(0)
        by_row_k = by_row_tile(1)
        for by_row, turned in ((by_row_q, turned_q), (by_row_k, turned_k)):
            for w in range(WINDOWS):
                sort_rows(nc.scalar.copy, by_row, turned, w, (0, RUNS))

        v_sums = [[bank(V_BANKS[w][0]), None] for w in range(WINDOWS)]
        for pass0, passes, parts in V_LOADS:
            column0 = V_PARTS[parts[0]][0]
            words = load_w(pass0, passes, QK_COLUMNS + column0, sum(V_PARTS[part][1] for part in parts))
            for part in parts:
                first, width = V_PARTS[part]
                if pass0 == 0 and part == 1:
                    for w in range(WINDOWS):
                        v_sums[w][1] = bank(V_BANKS[w][1])
                for w in range(WINDOWS):
                    for i in range(passes):
                        multiply(
                            pass0 + i,
                            w,
                            v_sums[w][part][:, :width],
                            words[:, i, first - column0 : first - column0 + width],
                            QK_COLUMNS + first,
                        )
        store(nc, by_row_q, out_0)
        store(nc, by_row_k, out_1)

        v_pieces = [
            [[(first, v_sums[w][part][:, :width])] for part, (first, width) in enumerate(V_PARTS)]
            for w in range(WINDOWS)
        ]
        y_v = work.tile(
            [P, WINDOWS, HEAD_DIM, HEADS], F32, tag="straight0", name="y_v", align_bytes=ALIGN
        )
        turned_v = turned_tile(2)
        by_row_v = by_row_tile(2)
        for w in range(WINDOWS):
            for axis in range(AXES):
                add_bias(nc, axis, w, y_v, v_pieces[w][0], bias_all[:, 2])
        for w in range(WINDOWS):
            for axis in range(AXES):
                add_bias(nc, axis, w, y_v, v_pieces[w][1], bias_all[:, 2])
            nc.vector.transpose(
                out=turned_v[:, w].rearrange("p e t -> p (e t)"),
                in_=y_v[:, w].rearrange("p e h -> p (e h)"),
            )
            if w == 0:
                sort_rows(nc.scalar.copy, by_row_v, turned_v, w, (0, RUNS))
        sort_rows(nc.scalar.copy, by_row_v, turned_v, 1, (0, RUNS // 3))
        sort_rows(nc.vector.tensor_copy, by_row_v, turned_v, 1, (RUNS // 3, RUNS))
        store(nc, by_row_v, out_2)
